import numpy as np
import ml_dtypes


def mxq(x, axis, fmt="e4m3"):
    dtype, down = {"e4m3": (ml_dtypes.float8_e4m3fn, 7), "e5m2": (ml_dtypes.float8_e5m2, 14)}[fmt]
    v = np.moveaxis(np.asarray(x, np.float32).astype(ml_dtypes.bfloat16).astype(np.float64), axis, -1)
    blocks = v.reshape(v.shape[:-1] + (-1, 32))
    amax = np.abs(blocks).max(-1, keepdims=True)
    byte = np.maximum(np.where(amax > 0, np.frexp(amax)[1] - 1 + 127, 0) - down, 1)
    scale = np.exp2(byte - 127.0)
    codes = (blocks / scale).astype(np.float32).astype(dtype).astype(np.float64)
    return np.moveaxis((codes * scale).reshape(v.shape), -1, axis)


WIDE = False


def mx_kscale(k):
    if not WIDE:
        return np.ones(k)
    levels = np.array([10, -10, 5, -5, 0])
    if k % 512:
        return np.exp2(np.random.permutation(np.resize(levels, k // 32))).repeat(32)
    a = np.empty((k // 512, 16))
    for p in range(k // 512):
        a[p, :8] = np.random.permutation(np.resize(levels, 8))
        for g in range(8):
            far = levels[np.abs(levels - a[p, g]) >= 10]
            a[p, g + 8] = far[np.random.randint(len(far))]
    return np.exp2(a.ravel()).repeat(32)


BF16 = ml_dtypes.bfloat16


def bf(x):
    return np.asarray(x, np.float32).astype(BF16)


def f64(x):
    return np.asarray(x).astype(np.float64)


B, T, C, A, H = 4, 256, 1024, 1024, 16


def sigmoid(v):
    return 1.0 / (1.0 + np.exp(-v))


def setup_inputs():
    s, t = mx_kscale(C), mx_kscale(A)
    return {"x": bf(np.random.standard_normal((B, T, C)) * s),
            "time_mix": bf(np.random.uniform(0.0, 1.0, (1, 1, C))),
            "Wr": bf(np.random.standard_normal((A, C)) * 1.5 / np.sqrt(C) / s[None, :]),
            "wkv": bf(np.random.standard_normal((B, T, A)) * 1.3 * t),
            "sum_k": bf(np.exp(1.0 + 0.6 * np.random.standard_normal((B, T, A)))),
            "Wo": bf(np.random.standard_normal((C, A)) * 1.5 / np.sqrt(A) / t[None, :])}


def reference(x, time_mix, Wr, wkv, sum_k, Wo):
    x, tm = f64(x), f64(time_mix)
    xs = np.concatenate([np.zeros_like(x[:, :1]), x[:, :-1]], axis=1)
    xm = x * tm + xs * (1.0 - tm)
    r = mxq(xm, 2, "e4m3") @ mxq(f64(Wr), 1, "e4m3").T
    g = sigmoid(r) * f64(wkv) / f64(sum_k)
    return mxq(g, 2, "e4m3") @ mxq(f64(Wo), 1, "e4m3").T

@@ -1,0 +1,321 @@
+import concourse.mybir as mybir
+from concourse.masks import make_identity
+
+F32 = mybir.dt.float32
+BF16 = mybir.dt.bfloat16
+U32 = mybir.dt.uint32
+U8 = mybir.dt.uint8
+FP8X4 = mybir.dt.float8_e4m3fn_x4
+ACT = mybir.ActivationFunctionType
+ALU = mybir.AluOpType
+
+P = 128
+TOKENS = 1024
+SEQ = 256
+CH = 1024
+PASSES = 2
+BLOCKS = 4
+HALF = 512
+N_TILES = TOKENS // P
+PAD = 8
+
+FLOPS = 2 * 2 * TOKENS * CH * CH
+
+
+def tile_rwkv2timemix_pa_kernel(tc, x, time_mix, Wr, wkv, sum_k, Wo, out):
+    nc = tc.nc
+    x_rows = x.flatten_outer_dims()
+    wkv_rows = wkv.flatten_outer_dims()
+    sum_k_rows = sum_k.flatten_outer_dims()
+    out_rows = out.flatten_outer_dims()
+
+    with tc.tile_pool(name="consts", bufs=1) as consts, tc.tile_pool(
+        name="inputs", bufs=4
+    ) as inputs, tc.tile_pool(name="keep", bufs=1) as keep, tc.tile_pool(
+        name="work", bufs=4
+    ) as work, tc.psum_pool(name="psum", bufs=8) as psum, tc.manual_schedule():
+        ones = consts.tile([P, 1], F32, name="ones")
+        nc.vector.memset(ones[:], 1.0)
+        warm = consts.tile([P, 1], F32, name="warm")
+        nc.scalar.activation(out=warm[:], in_=ones[:], func=ACT.Abs_reciprocal_sqrt)
+        ident = consts.tile([P, P], F32, name="ident")
+        make_identity(nc, ident[:])
+        tm_pairs = consts.tile([P, PASSES, 4], BF16, name="tm_pairs")
+        nc.scalar.dma_start(
+            out=tm_pairs[:], in_=time_mix.squeeze().rearrange("(c p t) -> p c t", p=P, t=4)
+        )
+        tm_col = consts.tile([P, 2 * BLOCKS], F32, name="tm_col")
+        nc.vector.tensor_copy(out=tm_col[:], in_=tm_pairs[:].rearrange("p c t -> p (c t)"))
+        rest_col = consts.tile([P, 2 * BLOCKS], F32, name="rest_col")
+        nc.vector.tensor_scalar(
+            out=rest_col[:], in0=tm_col[:], scalar1=-1.0, scalar2=1.0, op0=ALU.mult, op1=ALU.add
+        )
+        tm_diag = consts.tile([P, 2 * BLOCKS, P], BF16, name="tm_diag")
+        for col in range(2 * BLOCKS):
+            nc.vector.tensor_scalar_mul(out=tm_diag[:, col, :], in0=ident[:], scalar1=tm_col[:, col : col + 1])
+
+        def load_pair(rows, n, name):
+            pair = inputs.tile([P, 2, CH], BF16, name=name + str(n), tag=name)
+            nc.sync.dma_start(
+                out=pair[:], in_=rows[2 * P * n : 2 * P * (n + 1), :].rearrange("(i p) c -> p i c", p=P)
+            )
+            return pair
+
+        def load_wr(j):
+            pair = inputs.tile([P, 2, CH], BF16, name="wr" + str(j), tag="wr")
+            rows = Wr[HALF * (j // 2) : HALF * (j // 2 + 1), :].rearrange("(p t) c -> p t c", t=4)
+            nc.sync.dma_start(out=pair[:], in_=rows[:, 2 * (j % 2) : 2 * (j % 2) + 2, :])
+            return pair
+
+        def load_x(half, c):
+            tokens = inputs.tile([P, 4, HALF], BF16, name="x" + str(half) + str(c), tag="x")
+            for b in range(2):
+                first = HALF * half + SEQ * b
+                nc.sync.dma_start(
+                    out=tokens[:, 2 * b : 2 * b + 2, :],
+                    in_=x_rows[first : first + SEQ, HALF * c : HALF * (c + 1)].rearrange("(k p) c -> p k c", p=P),
+                )
+            return tokens
+
+        x_sb = [load_x(0, n) for n in range(2)]
+        sk_sb = [load_pair(sum_k_rows, n, "sk") for n in range(2)]
+        wr_sb = [load_wr(j) for j in range(2)]
+        wkv_sb = [load_pair(wkv_rows, 0, "wkv")]
+        wr_sb.extend([load_wr(j) for j in range(2, 4)])
+        wkv_sb.append(load_pair(wkv_rows, 1, "wkv"))
+        x_sb.extend([load_x(1, n) for n in range(2)])
+        sk_sb.extend([load_pair(sum_k_rows, n, "sk") for n in range(2, 4)])
+        wkv_sb.extend([load_pair(wkv_rows, n, "wkv") for n in range(2, 4)])
+        wo_sb = [load_pair(Wo, n, "wo") for n in range(4)]
+
+        x_codes = keep.tile([P, 2, PASSES, HALF], U32, name="x_codes", align_bytes=64)
+        x_scales = keep.tile([P, 2, PASSES, HALF], U8, name="x_scales", align_bytes=64)
+        wr_codes = keep.tile([P, 4, PASSES, 2 * P], U32, name="wr_codes", align_bytes=64)
+        wr_scales = keep.tile([P, 4, PASSES, 2 * P], U8, name="wr_scales", align_bytes=64)
+        wo_codes = keep.tile([P, PASSES, CH], U32, name="wo_codes", align_bytes=64)
+        wo_scales = keep.tile([P, PASSES, CH], U8, name="wo_scales", align_bytes=64)
+        g_codes = keep.tile([P, N_TILES, PASSES, P], U32, name="g_codes", align_bytes=64)
+        g_scales = keep.tile([P, N_TILES, PASSES, P], U8, name="g_scales", align_bytes=64)
+
+        def quantise(grouped, codes, scales):
+            nc.vector.quantize_mx(out=codes.bitcast(FP8X4), scales=scales, in_=grouped)
+
+        xt = keep.tile([P, BLOCKS, 2, PAD + SEQ], F32, name="xt")
+        xt_pairs = xt[:].bitcast(BF16).rearrange("p h s (k e) -> p h s k e", e=2)
+        nc.vector.memset(xt_pairs[:, :, :, 0:PAD, :], 0.0)
+
+        def transpose_x(half, h):
+            bank = psum.tile([P, 2, SEQ], F32, name="x_bank", tag="bank")
+            for k in range(4):
+                words = x_sb[2 * half + h // 2][:, k, :].bitcast(F32)
+                nc.tensor.transpose(bank[:, k // 2, P * (k % 2) : P * (k % 2 + 1)], words[:, h % 2 : 2 * P : 2], ident[:])
+            nc.scalar.copy(out=xt[:, h, :, PAD : PAD + SEQ], in_=bank[:])
+
+        def mix_block(planes, h):
+            for e in range(2):
+                col = 2 * h + e
+                scaled = psum.tile([P, 2, SEQ], F32, name="x_scaled", tag="bank")
+                nc.tensor.matmul(
+                    out=scaled[:],
+                    lhsT=tm_diag[:, col, :],
+                    rhs=xt_pairs[:, h, :, PAD : PAD + SEQ, e],
+                    start=True,
+                    stop=True,
+                )
+                nc.vector.scalar_tensor_tensor(
+                    out=planes[:, col, :].rearrange("p (s k) -> p s k", s=2),
+                    in0=xt_pairs[:, h, :, PAD - 1 : PAD - 1 + SEQ, e],
+                    scalar=rest_col[:, col : col + 1],
+                    in1=scaled[:],
+                    op0=ALU.mult,
+                    op1=ALU.add,
+                )
+
+        def mix_half(half):
+            planes = work.tile([P, 2 * BLOCKS, HALF], BF16, name="xm_planes", tag="planes")
+            for h in range(BLOCKS + 1):
+                if h < BLOCKS:
+                    transpose_x(half, h)
+                if h >= 1:
+                    mix_block(planes, h - 1)
+            groups = []
+            for c in range(PASSES):
+                grouped = work.tile([P, 4 * HALF], BF16, name="x_grouped", tag="grouped", align_bytes=64)
+                nc.vector.tensor_copy(
+                    out=grouped[:].rearrange("p (n i t) -> p n t i", i=4, t=4),
+                    in_=planes[:, 4 * c : 4 * (c + 1), :].rearrange("p t (n i) -> p n t i", i=4),
+                )
+                groups.append(grouped)
+            for c in range(PASSES):
+                quantise(groups[c][:], x_codes[:, half, c, :], x_scales[:, half, c, :])
+
+        def weight_bank(pair, c, grouped_words, copy):
+            bank = psum.tile([P, 2, 2 * P], F32, name="w_bank", tag="bank")
+            for u in range(2):
+                for m in range(2):
+                    words = pair[:, m, :].bitcast(F32)
+                    nc.tensor.transpose(
+                        bank[:, u, P * m : P * (m + 1)], words[:, 2 * P * c + u : 2 * P * (c + 1) : 2], ident[:]
+                    )
+            copy(out=grouped_words, in_=bank[:].rearrange("p u n -> p n u"))
+
+        def group_wr(j):
+            grouped = work.tile([P, 4 * HALF], BF16, name="wr_grouped", tag="grouped", align_bytes=64)
+            words = grouped[:].bitcast(F32).rearrange("p (c n u) -> p c n u", c=PASSES, u=2)
+            for c in range(PASSES):
+                weight_bank(wr_sb[j], c, words[:, c, :, :], nc.vector.tensor_copy)
+            return grouped
+
+        def quantise_wr(j, grouped):
+            quantise(
+                grouped[:],
+                wr_codes[:, j, :, :].rearrange("p c n -> p (c n)"),
+                wr_scales[:, j, :, :].rearrange("p c n -> p (c n)"),
+            )
+
+        def quantise_wo(half, c):
+            grouped = work.tile([P, 4 * HALF], BF16, name="wo_grouped", tag="grouped", align_bytes=64)
+            words = grouped[:].bitcast(F32).rearrange("p (m n u) -> p m n u", m=2, u=2)
+            for m in range(2):
+                weight_bank(wo_sb[2 * half + m], c, words[:, m, :, :], nc.scalar.copy)
+            cols = slice(HALF * half, HALF * (half + 1))
+            quantise(grouped[:], wo_codes[:, c, cols], wo_scales[:, c, cols])
+
+        root = []
+        ratio = []
+
+        def reciprocal_root(i):
+            r = keep.tile([P, CH], F32, name="root" + str(i))
+            nc.scalar.activation(out=r[:], in_=sk_sb[i // 2][:, i % 2, :], func=ACT.Abs_reciprocal_sqrt)
+            root.append(r)
+
+        def square(i):
+            nc.scalar.activation(out=root[i][:], in_=root[i][:], func=ACT.Square)
+
+        def divide(i, engine):
+            q = inputs.tile([P, PASSES, 4, P], F32, name="ratio" + str(i), tag=("x" if i % 4 < 2 else "sk"))
+            engine.tensor_tensor(
+                out=q[:],
+                in0=wkv_sb[i // 2][:, i % 2, :].rearrange("p (c k t) -> p c t k", c=PASSES, t=4),
+                in1=root[i][:].rearrange("p (c k t) -> p c t k", c=PASSES, t=4),
+                op=ALU.mult,
+            )
+            ratio.append(q)
+
+        gates = []
+
+        def receptance(s):
+            sig = work.tile([P, 2 * BLOCKS, SEQ], F32, name="sig", tag="planes")
+            cols = slice(SEQ * (s % 2), SEQ * (s % 2 + 1))
+            for j in range(BLOCKS):
+                acc = psum.tile([P, 2, SEQ], F32, name="r_acc", tag="bank")
+                for e in range(2):
+                    for c in range(PASSES):
+                        nc.tensor.matmul_mx(
+                            out=acc[:, e, :],
+                            lhsT=wr_codes[:, j, c, P * e : P * (e + 1)].bitcast(FP8X4),
+                            lhsT_scale=wr_scales[:, j, c, P * e : P * (e + 1)],
+                            rhs=x_codes[:, s // 2, c, cols].bitcast(FP8X4),
+                            rhs_scale=x_scales[:, s // 2, c, cols],
+                            start=(c == 0),
+                            stop=(c == PASSES - 1),
+                        )
+                nc.scalar.activation(out=sig[:, 2 * j : 2 * j + 2, :], in_=acc[:], func=ACT.Sigmoid)
+            gates.append(sig)
+
+        ratio_banks = []
+
+        def transpose_ratio(i):
+            banks = []
+            for c2 in range(PASSES):
+                bank = psum.tile([P, 4, P], F32, name="q_bank", tag="bank")
+                for t in range(4):
+                    nc.tensor.transpose(bank[:, t, :], ratio[i][:, c2, t, :], ident[:])
+                banks.append(bank)
+            ratio_banks.append(banks)
+
+        g_grouped = []
+
+        def gate(i):
+            grouped = work.tile([P, PASSES, P, 4], BF16, name="g_grouped", tag="g_grouped", align_bytes=64)
+            cols = slice(P * (i % 2), P * (i % 2 + 1))
+            for c2 in range(PASSES):
+                nc.vector.tensor_tensor(
+                    out=grouped[:, c2, :, :],
+                    in0=gates[i // 2][:, 4 * c2 : 4 * (c2 + 1), cols].rearrange("p t k -> p k t"),
+                    in1=ratio_banks[i][c2][:].rearrange("p t k -> p k t"),
+                    op=ALU.mult,
+                )
+            g_grouped.append(grouped)
+
+        def quantise_g(i):
+            quantise(
+                g_grouped[i][:].rearrange("p c k t -> p (c k t)"),
+                g_codes[:, i, :, :].rearrange("p c k -> p (c k)"),
+                g_scales[:, i, :, :].rearrange("p c k -> p (c k)"),
+            )
+
+        def project(i):
+            result = inputs.tile([P, CH], F32, name="result", tag="wr")
+            for half in range(2):
+                cols = slice(HALF * half, HALF * (half + 1))
+                acc = psum.tile([P, HALF], F32, name="o_acc", tag="bank")
+                for c2 in range(PASSES):
+                    nc.tensor.matmul_mx(
+                        out=acc[:],
+                        lhsT=g_codes[:, i, c2, :].bitcast(FP8X4),
+                        lhsT_scale=g_scales[:, i, c2, :],
+                        rhs=wo_codes[:, c2, cols].bitcast(FP8X4),
+                        rhs_scale=wo_scales[:, c2, cols],
+                        start=(c2 == 0),
+                        stop=(c2 == PASSES - 1),
+                    )
+                nc.scalar.copy(out=result[:, cols], in_=acc[:])
+                nc.sync.dma_start(out=out_rows[P * i : P * (i + 1), cols], in_=result[:, cols])
+
+        mix_half(0)
+        wr_grouped = []
+        for j in range(4 + 1):
+            if j < 4:
+                wr_grouped.append(group_wr(j))
+            if j >= 1:
+                quantise_wr(j - 1, wr_grouped[j - 1])
+        for n in range(2):
+            reciprocal_root(2 * n)
+            reciprocal_root(2 * n + 1)
+            for i in (2 * n, 2 * n + 1):
+                square(i)
+                divide(i, nc.gpsimd)
+        mix_half(1)
+        for i in range(4, N_TILES):
+            reciprocal_root(i)
+        receptance(0)
+        receptance(1)
+        for i in range(4, N_TILES):
+            square(i)
+        for i in range(4):
+            transpose_ratio(i)
+            gate(i)
+            if i >= 1:
+                quantise_g(i - 1)
+        quantise_g(3)
+        for i in range(4, N_TILES):
+            divide(i, nc.vector)
+        for half in range(2):
+            for c in range(PASSES):
+                quantise_wo(half, c)
+        receptance(2)
+        receptance(3)
+        transpose_ratio(4)
+        transpose_ratio(5)
+        for i in range(4):
+            project(i)
+        transpose_ratio(6)
+        transpose_ratio(7)
+        for i in range(4, N_TILES):
+            gate(i)
+            if i >= 5:
+                quantise_g(i - 1)
+                project(i - 1)
+        quantise_g(N_TILES - 1)
+        project(N_TILES - 1)

@@ -193,11 +193,11 @@ def tile_rwkv2timemix_pa_kernel(tc, x, time_mix, Wr, wkv, sum_k, Wo, out):
             nc.scalar.activation(out=root[i][:], in_=root[i][:], func=ACT.Square)
 
         def divide(i, engine):
-            q = inputs.tile([P, PASSES, 4, P], F32, name="ratio" + str(i), tag=("x" if i % 4 < 2 else "sk"))
+            q = inputs.tile([P, 4, PASSES, P], F32, name="ratio" + str(i), tag=("x" if i % 4 < 2 else "sk"))
             engine.tensor_tensor(
-                out=q[:],
-                in0=wkv_sb[i // 2][:, i % 2, :].rearrange("p (c k t) -> p c t k", c=PASSES, t=4),
-                in1=root[i][:].rearrange("p (c k t) -> p c t k", c=PASSES, t=4),
+                out=q[:].rearrange("p t c (n i) -> p (c n) t i", i=4),
+                in0=wkv_sb[i // 2][:, i % 2, :].rearrange("p (n i t) -> p n t i", i=4, t=4),
+                in1=root[i][:].rearrange("p (n i t) -> p n t i", i=4, t=4),
                 op=ALU.mult,
             )
             ratio.append(q)
@@ -230,7 +230,7 @@ def tile_rwkv2timemix_pa_kernel(tc, x, time_mix, Wr, wkv, sum_k, Wo, out):
             for c2 in range(PASSES):
                 bank = psum.tile([P, 4, P], F32, name="q_bank", tag="bank")
                 for t in range(4):
-                    nc.tensor.transpose(bank[:, t, :], ratio[i][:, c2, t, :], ident[:])
+                    nc.tensor.transpose(bank[:, t, :], ratio[i][:, t, c2, :], ident[:])
                 banks.append(bank)
             ratio_banks.append(banks)
 
@@ -241,9 +241,9 @@ def tile_rwkv2timemix_pa_kernel(tc, x, time_mix, Wr, wkv, sum_k, Wo, out):
             cols = slice(P * (i % 2), P * (i % 2 + 1))
             for c2 in range(PASSES):
                 nc.vector.tensor_tensor(
-                    out=grouped[:, c2, :, :],
-                    in0=gates[i // 2][:, 4 * c2 : 4 * (c2 + 1), cols].rearrange("p t k -> p k t"),
-                    in1=ratio_banks[i][c2][:].rearrange("p t k -> p k t"),
+                    out=grouped[:, c2, :, :].rearrange("p (n i) t -> p n t i", i=4),
+                    in0=gates[i // 2][:, 4 * c2 : 4 * (c2 + 1), cols].rearrange("p t (n i) -> p n t i", i=4),
+                    in1=ratio_banks[i][c2][:].rearrange("p t (n i) -> p n t i", i=4),
                     op=ALU.mult,
                 )
             g_grouped.append(grouped)

@@ -14,7 +14,6 @@ TOKENS = 1024
 SEQ = 256
 CH = 1024
 PASSES = 2
-BLOCKS = 4
 HALF = 512
 N_TILES = TOKENS // P
 PAD = 8
@@ -33,26 +32,17 @@ def tile_rwkv2timemix_pa_kernel(tc, x, time_mix, Wr, wkv, sum_k, Wo, out):
         name="inputs", bufs=4
     ) as inputs, tc.tile_pool(name="keep", bufs=1) as keep, tc.tile_pool(
         name="work", bufs=4
-    ) as work, tc.psum_pool(name="psum", bufs=8) as psum, tc.manual_schedule():
+    ) as work, tc.psum_pool(name="psum", bufs=4) as psum, tc.manual_schedule():
         ones = consts.tile([P, 1], F32, name="ones")
         nc.vector.memset(ones[:], 1.0)
-        warm = consts.tile([P, 1], F32, name="warm")
-        nc.scalar.activation(out=warm[:], in_=ones[:], func=ACT.Abs_reciprocal_sqrt)
         ident = consts.tile([P, P], F32, name="ident")
         make_identity(nc, ident[:])
         tm_pairs = consts.tile([P, PASSES, 4], BF16, name="tm_pairs")
         nc.scalar.dma_start(
             out=tm_pairs[:], in_=time_mix.squeeze().rearrange("(c p t) -> p c t", p=P, t=4)
         )
-        tm_col = consts.tile([P, 2 * BLOCKS], F32, name="tm_col")
-        nc.vector.tensor_copy(out=tm_col[:], in_=tm_pairs[:].rearrange("p c t -> p (c t)"))
-        rest_col = consts.tile([P, 2 * BLOCKS], F32, name="rest_col")
-        nc.vector.tensor_scalar(
-            out=rest_col[:], in0=tm_col[:], scalar1=-1.0, scalar2=1.0, op0=ALU.mult, op1=ALU.add
-        )
-        tm_diag = consts.tile([P, 2 * BLOCKS, P], BF16, name="tm_diag")
-        for col in range(2 * BLOCKS):
-            nc.vector.tensor_scalar_mul(out=tm_diag[:, col, :], in0=ident[:], scalar1=tm_col[:, col : col + 1])
+        warm = consts.tile([P, 1], F32, name="warm")
+        nc.scalar.activation(out=warm[:], in_=ones[:], func=ACT.Abs_reciprocal_sqrt)
 
         def load_pair(rows, n, name):
             pair = inputs.tile([P, 2, CH], BF16, name=name + str(n), tag=name)
@@ -69,24 +59,37 @@ def tile_rwkv2timemix_pa_kernel(tc, x, time_mix, Wr, wkv, sum_k, Wo, out):
 
         def load_x(half, c):
             tokens = inputs.tile([P, 4, HALF], BF16, name="x" + str(half) + str(c), tag="x")
-            for b in range(2):
-                first = HALF * half + SEQ * b
-                nc.sync.dma_start(
-                    out=tokens[:, 2 * b : 2 * b + 2, :],
-                    in_=x_rows[first : first + SEQ, HALF * c : HALF * (c + 1)].rearrange("(k p) c -> p k c", p=P),
-                )
+            nc.sync.dma_start(
+                out=tokens[:],
+                in_=x_rows[HALF * half : HALF * (half + 1), HALF * c : HALF * (c + 1)].rearrange(
+                    "(k p) c -> p k c", p=P
+                ),
+            )
             return tokens
 
-        x_sb = [load_x(0, n) for n in range(2)]
-        sk_sb = [load_pair(sum_k_rows, n, "sk") for n in range(2)]
-        wr_sb = [load_wr(j) for j in range(2)]
-        wkv_sb = [load_pair(wkv_rows, 0, "wkv")]
-        wr_sb.extend([load_wr(j) for j in range(2, 4)])
-        wkv_sb.append(load_pair(wkv_rows, 1, "wkv"))
-        x_sb.extend([load_x(1, n) for n in range(2)])
-        sk_sb.extend([load_pair(sum_k_rows, n, "sk") for n in range(2, 4)])
-        wkv_sb.extend([load_pair(wkv_rows, n, "wkv") for n in range(2, 4)])
-        wo_sb = [load_pair(Wo, n, "wo") for n in range(4)]
+        wr_sb, x_sb, sk_sb, wkv_sb, wo_sb = {}, {}, {}, {}, {}
+        for n in range(2):
+            for c in range(PASSES):
+                x_sb[n, c] = load_x(n, c)
+            sk_sb[n] = load_pair(sum_k_rows, n, "sk")
+        for n in range(2):
+            for j in (2 * n, 2 * n + 1):
+                wr_sb[j] = load_wr(j)
+            sk_sb[n + 2] = load_pair(sum_k_rows, n + 2, "sk")
+        for j in range(4):
+            wo_sb[j] = load_pair(Wo, j, "wo")
+        for n in range(4):
+            wkv_sb[n] = load_pair(wkv_rows, n, "wkv")
+
+        tm_col = consts.tile([P, 2 * 4], F32, name="tm_col")
+        nc.vector.tensor_copy(out=tm_col[:], in_=tm_pairs[:].rearrange("p c t -> p (c t)"))
+        rest_col = consts.tile([P, 2 * 4], F32, name="rest_col")
+        nc.vector.tensor_scalar(
+            out=rest_col[:], in0=tm_col[:], scalar1=-1.0, scalar2=1.0, op0=ALU.mult, op1=ALU.add
+        )
+        tm_diag = consts.tile([P, 2 * 4, P], BF16, name="tm_diag")
+        for col in range(2 * 4):
+            nc.vector.tensor_scalar_mul(out=tm_diag[:, col, :], in0=ident[:], scalar1=tm_col[:, col : col + 1])
 
         x_codes = keep.tile([P, 2, PASSES, HALF], U32, name="x_codes", align_bytes=64)
         x_scales = keep.tile([P, 2, PASSES, HALF], U8, name="x_scales", align_bytes=64)
@@ -100,71 +103,90 @@ def tile_rwkv2timemix_pa_kernel(tc, x, time_mix, Wr, wkv, sum_k, Wo, out):
         def quantise(grouped, codes, scales):
             nc.vector.quantize_mx(out=codes.bitcast(FP8X4), scales=scales, in_=grouped)
 
-        xt = keep.tile([P, BLOCKS, 2, PAD + SEQ], F32, name="xt")
-        xt_pairs = xt[:].bitcast(BF16).rearrange("p h s (k e) -> p h s k e", e=2)
-        nc.vector.memset(xt_pairs[:, :, :, 0:PAD, :], 0.0)
+        xt_pairs = []
+        xt_words = []
+        for half in range(2):
+            xt = keep.tile([P, PASSES, 2, 2, PAD + SEQ], F32, name="xt" + str(half))
+            xt_words.append(xt)
+            xt_pairs.append(xt[:].bitcast(BF16).rearrange("p c u s (k e) -> p c u s k e", e=2))
+            nc.vector.memset(xt_pairs[half][:, :, :, :, 0:PAD, :], 0.0)
 
-        def transpose_x(half, h):
-            bank = psum.tile([P, 2, SEQ], F32, name="x_bank", tag="bank")
-            for k in range(4):
-                words = x_sb[2 * half + h // 2][:, k, :].bitcast(F32)
-                nc.tensor.transpose(bank[:, k // 2, P * (k % 2) : P * (k % 2 + 1)], words[:, h % 2 : 2 * P : 2], ident[:])
-            nc.scalar.copy(out=xt[:, h, :, PAD : PAD + SEQ], in_=bank[:])
+        def transpose_x(half, c):
+            banks = []
+            for u in range(2):
+                bank = psum.tile([P, 2, SEQ], F32, name="x_bank", tag="scalar_bank")
+                for k in range(4):
+                    words = x_sb[half, c][:, k, :].bitcast(F32)
+                    nc.tensor.transpose(bank[:, k // 2, P * (k % 2) : P * (k % 2 + 1)], words[:, u : 2 * P : 2], ident[:])
+                banks.append(bank)
+            return banks
 
-        def mix_block(planes, h):
-            for e in range(2):
-                col = 2 * h + e
-                scaled = psum.tile([P, 2, SEQ], F32, name="x_scaled", tag="bank")
+        def copy_x(half, c, banks):
+            for u in range(2):
+                nc.scalar.copy(out=xt_words[half][:, c, u, :, PAD : PAD + SEQ], in_=banks[u][:])
+
+        def scale_current(half, c):
+            banks = []
+            for t in range(4):
+                scaled = psum.tile([P, 2, SEQ], F32, name="x_scaled", tag="vector_bank")
                 nc.tensor.matmul(
                     out=scaled[:],
-                    lhsT=tm_diag[:, col, :],
-                    rhs=xt_pairs[:, h, :, PAD : PAD + SEQ, e],
+                    lhsT=tm_diag[:, 4 * c + t, :],
+                    rhs=xt_pairs[half][:, c, t // 2, :, PAD : PAD + SEQ, t % 2],
                     start=True,
                     stop=True,
                 )
+                banks.append(scaled)
+            return banks
+
+        def mix(half, c, banks):
+            planes = work.tile([P, 4, HALF], BF16, name="xm_planes", tag="planes")
+            for t in range(4):
                 nc.vector.scalar_tensor_tensor(
-                    out=planes[:, col, :].rearrange("p (s k) -> p s k", s=2),
-                    in0=xt_pairs[:, h, :, PAD - 1 : PAD - 1 + SEQ, e],
-                    scalar=rest_col[:, col : col + 1],
-                    in1=scaled[:],
+                    out=planes[:, t, :].rearrange("p (s k) -> p s k", s=2),
+                    in0=xt_pairs[half][:, c, t // 2, :, PAD - 1 : PAD - 1 + SEQ, t % 2],
+                    scalar=rest_col[:, 4 * c + t : 4 * c + t + 1],
+                    in1=banks[t][:],
                     op0=ALU.mult,
                     op1=ALU.add,
                 )
+            return planes
 
-        def mix_half(half):
-            planes = work.tile([P, 2 * BLOCKS, HALF], BF16, name="xm_planes", tag="planes")
-            for h in range(BLOCKS + 1):
-                if h < BLOCKS:
-                    transpose_x(half, h)
-                if h >= 1:
-                    mix_block(planes, h - 1)
-            groups = []
-            for c in range(PASSES):
-                grouped = work.tile([P, 4 * HALF], BF16, name="x_grouped", tag="grouped", align_bytes=64)
-                nc.vector.tensor_copy(
-                    out=grouped[:].rearrange("p (n i t) -> p n t i", i=4, t=4),
-                    in_=planes[:, 4 * c : 4 * (c + 1), :].rearrange("p t (n i) -> p n t i", i=4),
-                )
-                groups.append(grouped)
-            for c in range(PASSES):
-                quantise(groups[c][:], x_codes[:, half, c, :], x_scales[:, half, c, :])
+        def interleave(planes):
+            grouped = work.tile([P, HALF, 4], BF16, name="x_grouped", tag="grouped", align_bytes=64)
+            nc.vector.tensor_copy(
+                out=grouped[:].rearrange("p (n i) t -> p n t i", i=4),
+                in_=planes[:].rearrange("p t (n i) -> p n t i", i=4),
+            )
+            return grouped
 
-        def weight_bank(pair, c, grouped_words, copy):
-            bank = psum.tile([P, 2, 2 * P], F32, name="w_bank", tag="bank")
+        def quantise_x(half, c, grouped):
+            quantise(grouped[:].rearrange("p k t -> p (k t)"), x_codes[:, half, c, :], x_scales[:, half, c, :])
+
+        def transpose_weight(pair, c, tag):
+            bank = psum.tile([P, 2, 2 * P], F32, name="w_bank", tag=tag)
             for u in range(2):
                 for m in range(2):
                     words = pair[:, m, :].bitcast(F32)
                     nc.tensor.transpose(
                         bank[:, u, P * m : P * (m + 1)], words[:, 2 * P * c + u : 2 * P * (c + 1) : 2], ident[:]
                     )
-            copy(out=grouped_words, in_=bank[:].rearrange("p u n -> p n u"))
+            return bank
+
+        def group_weight(banks, copies):
+            grouped = work.tile([P, 4 * HALF], BF16, name="w_grouped", tag="grouped", align_bytes=64)
+            words = grouped[:].bitcast(F32).rearrange("p (b n u) -> p b n u", b=2, u=2)
+            for b in range(2):
+                copies[b](out=words[:, b, :, :], in_=banks[b][:].rearrange("p u n -> p n u"))
+            return grouped
 
         def group_wr(j):
-            grouped = work.tile([P, 4 * HALF], BF16, name="wr_grouped", tag="grouped", align_bytes=64)
-            words = grouped[:].bitcast(F32).rearrange("p (c n u) -> p c n u", c=PASSES, u=2)
-            for c in range(PASSES):
-                weight_bank(wr_sb[j], c, words[:, c, :, :], nc.vector.tensor_copy)
-            return grouped
+            banks = [transpose_weight(wr_sb[j], c, "scalar_bank") for c in range(PASSES)]
+            return group_weight(banks, [nc.scalar.copy, nc.scalar.copy])
+
+        def group_wo(half, c, tag, copy):
+            banks = [transpose_weight(wo_sb[2 * half + m], c, tag) for m in range(2)]
+            return group_weight(banks, [copy, copy])
 
         def quantise_wr(j, grouped):
             quantise(
@@ -173,42 +195,41 @@ def tile_rwkv2timemix_pa_kernel(tc, x, time_mix, Wr, wkv, sum_k, Wo, out):
                 wr_scales[:, j, :, :].rearrange("p c n -> p (c n)"),
             )
 
-        def quantise_wo(half, c):
-            grouped = work.tile([P, 4 * HALF], BF16, name="wo_grouped", tag="grouped", align_bytes=64)
-            words = grouped[:].bitcast(F32).rearrange("p (m n u) -> p m n u", m=2, u=2)
-            for m in range(2):
-                weight_bank(wo_sb[2 * half + m], c, words[:, m, :, :], nc.scalar.copy)
+        def quantise_wo(half, c, grouped):
             cols = slice(HALF * half, HALF * (half + 1))
             quantise(grouped[:], wo_codes[:, c, cols], wo_scales[:, c, cols])
 
-        root = []
-        ratio = []
+        root = {}
+        ratio = {}
 
         def reciprocal_root(i):
-            r = keep.tile([P, CH], F32, name="root" + str(i))
-            nc.scalar.activation(out=r[:], in_=sk_sb[i // 2][:, i % 2, :], func=ACT.Abs_reciprocal_sqrt)
-            root.append(r)
+            root[i] = keep.tile([P, 4, PASSES, P], F32, name="root" + str(i))
+            nc.scalar.activation(
+                out=root[i][:].rearrange("p t c (n i) -> p (c n) t i", i=4),
+                in_=sk_sb[i // 2][:, i % 2, :].rearrange("p (n i t) -> p n t i", i=4, t=4),
+                func=ACT.Abs_reciprocal_sqrt,
+            )
 
         def square(i):
             nc.scalar.activation(out=root[i][:], in_=root[i][:], func=ACT.Square)
 
-        def divide(i, engine):
-            q = inputs.tile([P, 4, PASSES, P], F32, name="ratio" + str(i), tag=("x" if i % 4 < 2 else "sk"))
-            engine.tensor_tensor(
-                out=q[:].rearrange("p t c (n i) -> p (c n) t i", i=4),
+        def divide(i):
+            ratio[i] = inputs.tile([P, 4, PASSES, P], F32, name="ratio" + str(i), tag=("x" if i % 4 < 2 else "sk"))
+            nc.vector.tensor_tensor(
+                out=ratio[i][:].rearrange("p t c (n i) -> p (c n) t i", i=4),
                 in0=wkv_sb[i // 2][:, i % 2, :].rearrange("p (n i t) -> p n t i", i=4, t=4),
-                in1=root[i][:].rearrange("p (n i t) -> p n t i", i=4, t=4),
+                in1=root[i][:].rearrange("p t c (n i) -> p (c n) t i", i=4),
                 op=ALU.mult,
             )
-            ratio.append(q)
 
-        gates = []
+        gates = {}
+        r_banks = {}
 
         def receptance(s):
-            sig = work.tile([P, 2 * BLOCKS, SEQ], F32, name="sig", tag="planes")
             cols = slice(SEQ * (s % 2), SEQ * (s % 2 + 1))
-            for j in range(BLOCKS):
-                acc = psum.tile([P, 2, SEQ], F32, name="r_acc", tag="bank")
+            r_banks[s] = []
+            for j in range(4):
+                acc = psum.tile([P, 2, SEQ], F32, name="r_acc", tag="scalar_bank")
                 for e in range(2):
                     for c in range(PASSES):
                         nc.tensor.matmul_mx(
@@ -220,21 +241,25 @@ def tile_rwkv2timemix_pa_kernel(tc, x, time_mix, Wr, wkv, sum_k, Wo, out):
                             start=(c == 0),
                             stop=(c == PASSES - 1),
                         )
-                nc.scalar.activation(out=sig[:, 2 * j : 2 * j + 2, :], in_=acc[:], func=ACT.Sigmoid)
-            gates.append(sig)
+                r_banks[s].append(acc)
 
-        ratio_banks = []
+        def sigmoid(s):
+            gates[s] = work.tile([P, 2 * 4, SEQ], F32, name="sig", tag="planes")
+            for j in range(4):
+                nc.scalar.activation(out=gates[s][:, 2 * j : 2 * j + 2, :], in_=r_banks[s][j][:], func=ACT.Sigmoid)
+
+        ratio_banks = {}
 
         def transpose_ratio(i):
             banks = []
             for c2 in range(PASSES):
-                bank = psum.tile([P, 4, P], F32, name="q_bank", tag="bank")
+                bank = psum.tile([P, 4, P], F32, name="q_bank", tag="vector_bank")
                 for t in range(4):
                     nc.tensor.transpose(bank[:, t, :], ratio[i][:, t, c2, :], ident[:])
                 banks.append(bank)
-            ratio_banks.append(banks)
+            ratio_banks[i] = banks
 
-        g_grouped = []
+        g_grouped = {}
 
         def gate(i):
             grouped = work.tile([P, PASSES, P, 4], BF16, name="g_grouped", tag="g_grouped", align_bytes=64)
@@ -246,7 +271,7 @@ def tile_rwkv2timemix_pa_kernel(tc, x, time_mix, Wr, wkv, sum_k, Wo, out):
                     in1=ratio_banks[i][c2][:].rearrange("p t (n i) -> p n t i", i=4),
                     op=ALU.mult,
                 )
-            g_grouped.append(grouped)
+            g_grouped[i] = grouped
 
         def quantise_g(i):
             quantise(
@@ -255,11 +280,13 @@ def tile_rwkv2timemix_pa_kernel(tc, x, time_mix, Wr, wkv, sum_k, Wo, out):
                 g_scales[:, i, :, :].rearrange("p c k -> p (c k)"),
             )
 
-        def project(i):
-            result = inputs.tile([P, CH], F32, name="result", tag="wr")
+        o_banks = {}
+
+        def project(i, tags):
+            o_banks[i] = []
             for half in range(2):
                 cols = slice(HALF * half, HALF * (half + 1))
-                acc = psum.tile([P, HALF], F32, name="o_acc", tag="bank")
+                acc = psum.tile([P, HALF], F32, name="o_acc", tag=tags[half])
                 for c2 in range(PASSES):
                     nc.tensor.matmul_mx(
                         out=acc[:],
@@ -270,52 +297,100 @@ def tile_rwkv2timemix_pa_kernel(tc, x, time_mix, Wr, wkv, sum_k, Wo, out):
                         start=(c2 == 0),
                         stop=(c2 == PASSES - 1),
                     )
-                nc.scalar.copy(out=result[:, cols], in_=acc[:])
+                o_banks[i].append(acc)
+
+        def store(i, copies):
+            result = inputs.tile([P, CH], F32, name="result", tag="wr")
+            for half in range(2):
+                cols = slice(HALF * half, HALF * (half + 1))
+                copies[half](out=result[:, cols], in_=o_banks[i][half][:])
                 nc.sync.dma_start(out=out_rows[P * i : P * (i + 1), cols], in_=result[:, cols])
 
-        mix_half(0)
-        wr_grouped = []
-        for j in range(4 + 1):
-            if j < 4:
-                wr_grouped.append(group_wr(j))
-            if j >= 1:
-                quantise_wr(j - 1, wr_grouped[j - 1])
-        for n in range(2):
-            reciprocal_root(2 * n)
-            reciprocal_root(2 * n + 1)
-            for i in (2 * n, 2 * n + 1):
-                square(i)
-                divide(i, nc.gpsimd)
-        mix_half(1)
+        copy_x(0, 0, transpose_x(0, 0))
+        copy_x(0, 1, transpose_x(0, 1))
+        planes00 = mix(0, 0, scale_current(0, 0))
+        reciprocal_root(0)
+        copy_x(1, 0, transpose_x(1, 0))
+        planes01 = mix(0, 1, scale_current(0, 1))
+        reciprocal_root(1)
+        copy_x(1, 1, transpose_x(1, 1))
+        x00 = interleave(planes00)
+        planes10 = mix(1, 0, scale_current(1, 0))
+        wr0 = group_wr(0)
+        quantise_x(0, 0, x00)
+        x01 = interleave(planes01)
+        wr1 = group_wr(1)
+        planes11 = mix(1, 1, scale_current(1, 1))
+        quantise_wr(0, wr0)
+        quantise_x(0, 1, x01)
+        square(0)
+        wr2 = group_wr(2)
+        quantise_wr(1, wr1)
+        square(1)
+        wr3 = group_wr(3)
+        x10 = interleave(planes10)
+        quantise_wr(2, wr2)
+        quantise_wr(3, wr3)
+        reciprocal_root(2)
+        reciprocal_root(3)
+        x11 = interleave(planes11)
+        quantise_x(1, 0, x10)
+        receptance(0)
+        divide(0)
+        quantise_x(1, 1, x11)
+        divide(1)
+        wo10 = group_wo(1, 0, "vector_bank", nc.vector.tensor_copy)
         for i in range(4, N_TILES):
             reciprocal_root(i)
-        receptance(0)
+        sigmoid(0)
+        wo11 = group_wo(1, 1, "vector_bank", nc.vector.tensor_copy)
+        quantise_wo(1, 0, wo10)
+        transpose_ratio(0)
+        transpose_ratio(1)
+        quantise_wo(1, 1, wo11)
         receptance(1)
-        for i in range(4, N_TILES):
-            square(i)
-        for i in range(4):
-            transpose_ratio(i)
-            gate(i)
-            if i >= 1:
-                quantise_g(i - 1)
-        quantise_g(3)
-        for i in range(4, N_TILES):
-            divide(i, nc.vector)
-        for half in range(2):
-            for c in range(PASSES):
-                quantise_wo(half, c)
+        square(2)
+        sigmoid(1)
+        gate(0)
+        gate(1)
+        wo00 = group_wo(0, 0, "scalar_bank", nc.scalar.copy)
+        divide(2)
+        quantise_g(0)
+        square(3)
+        wo01 = group_wo(0, 1, "scalar_bank", nc.scalar.copy)
+        quantise_g(1)
+        quantise_wo(0, 0, wo00)
+        divide(3)
+        quantise_wo(0, 1, wo01)
         receptance(2)
-        receptance(3)
-        transpose_ratio(4)
-        transpose_ratio(5)
-        for i in range(4):
-            project(i)
-        transpose_ratio(6)
-        transpose_ratio(7)
-        for i in range(4, N_TILES):
-            gate(i)
-            if i >= 5:
-                quantise_g(i - 1)
-                project(i - 1)
-        quantise_g(N_TILES - 1)
-        project(N_TILES - 1)
+        sigmoid(2)
+        transpose_ratio(2)
+        transpose_ratio(3)
+        gate(2)
+        gate(3)
+        square(4)
+        square(5)
+        for s in range(1, 4):
+            for i in (2 * s - 2, 2 * s - 1):
+                project(i, ["scalar_bank", "scalar_bank"])
+                store(i, [nc.scalar.copy, nc.scalar.copy])
+            if s < 3:
+                divide(2 * s + 2)
+                quantise_g(2 * s)
+                divide(2 * s + 3)
+                quantise_g(2 * s + 1)
+                if s == 1:
+                    receptance(3)
+                    sigmoid(3)
+                    square(6)
+                    square(7)
+                transpose_ratio(2 * s + 2)
+                transpose_ratio(2 * s + 3)
+                gate(2 * s + 2)
+                gate(2 * s + 3)
+            else:
+                quantise_g(6)
+                quantise_g(7)
+        for i in (6, 7):
+            project(i, ["scalar_bank", "vector_bank"])
+            store(i, [nc.scalar.copy, nc.vector.tensor_copy])

@@ -32,7 +32,9 @@ def tile_rwkv2timemix_pa_kernel(tc, x, time_mix, Wr, wkv, sum_k, Wo, out):
         name="inputs", bufs=4
     ) as inputs, tc.tile_pool(name="keep", bufs=1) as keep, tc.tile_pool(
         name="work", bufs=4
-    ) as work, tc.psum_pool(name="psum", bufs=4) as psum, tc.manual_schedule():
+    ) as work, tc.tile_pool(name="groups", bufs=6) as groups, tc.tile_pool(
+        name="gated", bufs=3
+    ) as gated, tc.psum_pool(name="psum", bufs=4) as psum, tc.manual_schedule():
         ones = consts.tile([P, 1], F32, name="ones")
         nc.vector.memset(ones[:], 1.0)
         ident = consts.tile([P, P], F32, name="ident")
@@ -57,27 +59,42 @@ def tile_rwkv2timemix_pa_kernel(tc, x, time_mix, Wr, wkv, sum_k, Wo, out):
             nc.sync.dma_start(out=pair[:], in_=rows[:, 2 * (j % 2) : 2 * (j % 2) + 2, :])
             return pair
 
-        def load_x(half, c):
-            tokens = inputs.tile([P, 4, HALF], BF16, name="x" + str(half) + str(c), tag="x")
-            nc.sync.dma_start(
-                out=tokens[:],
-                in_=x_rows[HALF * half : HALF * (half + 1), HALF * c : HALF * (c + 1)].rearrange(
-                    "(k p) c -> p k c", p=P
-                ),
-            )
-            return tokens
+        def load_x(half, c, pieces=1):
+            x_sb[half, c] = inputs.tile([P, 4, HALF], BF16, name="x" + str(half) + str(c), tag="x")
+            n = 4 // pieces
+            for k in range(0, 4, n):
+                rows = slice(HALF * half + P * k, HALF * half + P * (k + n))
+                nc.sync.dma_start(
+                    out=x_sb[half, c][:, k : k + n, :],
+                    in_=x_rows[rows, HALF * c : HALF * (c + 1)].rearrange("(k p) c -> p k c", p=P),
+                )
+
+        def load_sk(n, pieces=1):
+            sk_sb[n] = inputs.tile([P, 2, CH], BF16, name="sk" + str(n), tag="sk")
+            k = 2 // pieces
+            for i in range(0, 2, k):
+                rows = slice(P * (2 * n + i), P * (2 * n + i + k))
+                nc.sync.dma_start(
+                    out=sk_sb[n][:, i : i + k, :], in_=sum_k_rows[rows, :].rearrange("(i p) c -> p i c", p=P)
+                )
 
         wr_sb, x_sb, sk_sb, wkv_sb, wo_sb = {}, {}, {}, {}, {}
+        load_x(0, 0, 2)
+        load_sk(0, 2)
+        load_x(0, 1)
+        load_x(1, 0)
+        load_sk(1)
         for n in range(2):
-            for c in range(PASSES):
-                x_sb[n, c] = load_x(n, c)
-            sk_sb[n] = load_pair(sum_k_rows, n, "sk")
-        for n in range(2):
-            for j in (2 * n, 2 * n + 1):
-                wr_sb[j] = load_wr(j)
-            sk_sb[n + 2] = load_pair(sum_k_rows, n + 2, "sk")
-        for j in range(4):
-            wo_sb[j] = load_pair(Wo, j, "wo")
+            wo_sb[n] = load_pair(Wo, n, "wo")
+        load_x(1, 1)
+        for j in range(2):
+            wr_sb[j] = load_wr(j)
+        load_sk(2)
+        for j in range(2, 4):
+            wr_sb[j] = load_wr(j)
+        load_sk(3)
+        for n in range(2, 4):
+            wo_sb[n] = load_pair(Wo, n, "wo")
         for n in range(4):
             wkv_sb[n] = load_pair(wkv_rows, n, "wkv")
 
@@ -113,17 +130,18 @@ def tile_rwkv2timemix_pa_kernel(tc, x, time_mix, Wr, wkv, sum_k, Wo, out):
 
         def transpose_x(half, c):
             banks = []
-            for u in range(2):
+            for s in range(2):
                 bank = psum.tile([P, 2, SEQ], F32, name="x_bank", tag="scalar_bank")
-                for k in range(4):
-                    words = x_sb[half, c][:, k, :].bitcast(F32)
-                    nc.tensor.transpose(bank[:, k // 2, P * (k % 2) : P * (k % 2 + 1)], words[:, u : 2 * P : 2], ident[:])
+                for k in range(2):
+                    words = x_sb[half, c][:, 2 * s + k, :].bitcast(F32)
+                    for u in range(2):
+                        nc.tensor.transpose(bank[:, u, P * k : P * (k + 1)], words[:, u : 2 * P : 2], ident[:])
                 banks.append(bank)
             return banks
 
         def copy_x(half, c, banks):
-            for u in range(2):
-                nc.scalar.copy(out=xt_words[half][:, c, u, :, PAD : PAD + SEQ], in_=banks[u][:])
+            for s in range(2):
+                nc.scalar.copy(out=xt_words[half][:, c, :, s, PAD : PAD + SEQ], in_=banks[s][:])
 
         def scale_current(half, c):
             banks = []
@@ -153,7 +171,7 @@ def tile_rwkv2timemix_pa_kernel(tc, x, time_mix, Wr, wkv, sum_k, Wo, out):
             return planes
 
         def interleave(planes):
-            grouped = work.tile([P, HALF, 4], BF16, name="x_grouped", tag="grouped", align_bytes=64)
+            grouped = groups.tile([P, HALF, 4], BF16, name="x_grouped", tag="grouped", align_bytes=64)
             nc.vector.tensor_copy(
                 out=grouped[:].rearrange("p (n i) t -> p n t i", i=4),
                 in_=planes[:].rearrange("p t (n i) -> p n t i", i=4),
@@ -174,7 +192,7 @@ def tile_rwkv2timemix_pa_kernel(tc, x, time_mix, Wr, wkv, sum_k, Wo, out):
             return bank
 
         def group_weight(banks, copies):
-            grouped = work.tile([P, 4 * HALF], BF16, name="w_grouped", tag="grouped", align_bytes=64)
+            grouped = groups.tile([P, 4 * HALF], BF16, name="w_grouped", tag="grouped", align_bytes=64)
             words = grouped[:].bitcast(F32).rearrange("p (b n u) -> p b n u", b=2, u=2)
             for b in range(2):
                 copies[b](out=words[:, b, :, :], in_=banks[b][:].rearrange("p u n -> p n u"))
@@ -261,17 +279,16 @@ def tile_rwkv2timemix_pa_kernel(tc, x, time_mix, Wr, wkv, sum_k, Wo, out):
 
         g_grouped = {}
 
-        def gate(i):
-            grouped = work.tile([P, PASSES, P, 4], BF16, name="g_grouped", tag="g_grouped", align_bytes=64)
+        def gate(i, c2):
+            if c2 == 0:
+                g_grouped[i] = gated.tile([P, PASSES, P, 4], BF16, name="g_grouped", tag="g_grouped", align_bytes=64)
             cols = slice(P * (i % 2), P * (i % 2 + 1))
-            for c2 in range(PASSES):
-                nc.vector.tensor_tensor(
-                    out=grouped[:, c2, :, :].rearrange("p (n i) t -> p n t i", i=4),
-                    in0=gates[i // 2][:, 4 * c2 : 4 * (c2 + 1), cols].rearrange("p t (n i) -> p n t i", i=4),
-                    in1=ratio_banks[i][c2][:].rearrange("p t (n i) -> p n t i", i=4),
-                    op=ALU.mult,
-                )
-            g_grouped[i] = grouped
+            nc.vector.tensor_tensor(
+                out=g_grouped[i][:, c2, :, :].rearrange("p (n i) t -> p n t i", i=4),
+                in0=gates[i // 2][:, 4 * c2 : 4 * (c2 + 1), cols].rearrange("p t (n i) -> p n t i", i=4),
+                in1=ratio_banks[i][c2][:].rearrange("p t (n i) -> p n t i", i=4),
+                op=ALU.mult,
+            )
 
         def quantise_g(i):
             quantise(
@@ -306,91 +323,112 @@ def tile_rwkv2timemix_pa_kernel(tc, x, time_mix, Wr, wkv, sum_k, Wo, out):
                 copies[half](out=result[:, cols], in_=o_banks[i][half][:])
                 nc.sync.dma_start(out=out_rows[P * i : P * (i + 1), cols], in_=result[:, cols])
 
+        on_scalar = ("scalar_bank", nc.scalar.copy)
+        on_vector = ("vector_bank", nc.vector.tensor_copy)
         copy_x(0, 0, transpose_x(0, 0))
-        copy_x(0, 1, transpose_x(0, 1))
         planes00 = mix(0, 0, scale_current(0, 0))
         reciprocal_root(0)
+        reciprocal_root(1)
+        copy_x(0, 1, transpose_x(0, 1))
+        x00 = interleave(planes00)
+        square(0)
         copy_x(1, 0, transpose_x(1, 0))
         planes01 = mix(0, 1, scale_current(0, 1))
-        reciprocal_root(1)
-        copy_x(1, 1, transpose_x(1, 1))
-        x00 = interleave(planes00)
+        reciprocal_root(2)
+        wo00 = group_wo(0, 0, *on_scalar)
         planes10 = mix(1, 0, scale_current(1, 0))
-        wr0 = group_wr(0)
         quantise_x(0, 0, x00)
         x01 = interleave(planes01)
-        wr1 = group_wr(1)
+        copy_x(1, 1, transpose_x(1, 1))
+        wo01 = group_wo(0, 1, *on_scalar)
         planes11 = mix(1, 1, scale_current(1, 1))
-        quantise_wr(0, wr0)
+        square(1)
         quantise_x(0, 1, x01)
-        square(0)
+        quantise_wo(0, 0, wo00)
+        wr0 = group_wr(0)
+        x10 = interleave(planes10)
+        reciprocal_root(3)
+        wr1 = group_wr(1)
+        quantise_wo(0, 1, wo01)
+        quantise_wr(0, wr0)
         wr2 = group_wr(2)
         quantise_wr(1, wr1)
-        square(1)
-        wr3 = group_wr(3)
-        x10 = interleave(planes10)
-        quantise_wr(2, wr2)
-        quantise_wr(3, wr3)
-        reciprocal_root(2)
-        reciprocal_root(3)
-        x11 = interleave(planes11)
         quantise_x(1, 0, x10)
-        receptance(0)
+        reciprocal_root(4)
+        wr3 = group_wr(3)
+        x11 = interleave(planes11)
+        quantise_wr(2, wr2)
         divide(0)
+        quantise_wr(3, wr3)
         quantise_x(1, 1, x11)
         divide(1)
-        wo10 = group_wo(1, 0, "vector_bank", nc.vector.tensor_copy)
-        for i in range(4, N_TILES):
+        wo10 = group_wo(1, 0, *on_vector)
+        receptance(0)
+        for i in range(5, N_TILES):
             reciprocal_root(i)
-        sigmoid(0)
-        wo11 = group_wo(1, 1, "vector_bank", nc.vector.tensor_copy)
-        quantise_wo(1, 0, wo10)
         transpose_ratio(0)
         transpose_ratio(1)
-        quantise_wo(1, 1, wo11)
+        sigmoid(0)
+        gate(0, 0)
+        gate(0, 1)
         receptance(1)
+        quantise_wo(1, 0, wo10)
         square(2)
-        sigmoid(1)
-        gate(0)
-        gate(1)
-        wo00 = group_wo(0, 0, "scalar_bank", nc.scalar.copy)
-        divide(2)
+        gate(1, 0)
         quantise_g(0)
-        square(3)
-        wo01 = group_wo(0, 1, "scalar_bank", nc.scalar.copy)
+        gate(1, 1)
+        sigmoid(1)
+        wo11 = group_wo(1, 1, *on_vector)
+        divide(2)
         quantise_g(1)
-        quantise_wo(0, 0, wo00)
-        divide(3)
-        quantise_wo(0, 1, wo01)
+        square(3)
         receptance(2)
-        sigmoid(2)
+        quantise_wo(1, 1, wo11)
+        divide(3)
         transpose_ratio(2)
-        transpose_ratio(3)
-        gate(2)
-        gate(3)
         square(4)
+        sigmoid(2)
+        gate(2, 0)
+        gate(2, 1)
+        transpose_ratio(3)
         square(5)
-        for s in range(1, 4):
-            for i in (2 * s - 2, 2 * s - 1):
-                project(i, ["scalar_bank", "scalar_bank"])
-                store(i, [nc.scalar.copy, nc.scalar.copy])
-            if s < 3:
-                divide(2 * s + 2)
-                quantise_g(2 * s)
-                divide(2 * s + 3)
-                quantise_g(2 * s + 1)
-                if s == 1:
-                    receptance(3)
-                    sigmoid(3)
-                    square(6)
-                    square(7)
-                transpose_ratio(2 * s + 2)
-                transpose_ratio(2 * s + 3)
-                gate(2 * s + 2)
-                gate(2 * s + 3)
-            else:
-                quantise_g(6)
-                quantise_g(7)
+        gate(3, 0)
+        quantise_g(2)
+        gate(3, 1)
+        receptance(3)
+        square(6)
+        divide(4)
+        quantise_g(3)
+        divide(5)
+        sigmoid(3)
+        transpose_ratio(4)
+        transpose_ratio(5)
+        square(7)
+        for i in (0, 1):
+            project(i, ["scalar_bank", "scalar_bank"])
+            store(i, [nc.scalar.copy, nc.scalar.copy])
+        gate(4, 0)
+        gate(4, 1)
+        divide(6)
+        gate(5, 0)
+        quantise_g(4)
+        gate(5, 1)
+        divide(7)
+        quantise_g(5)
+        for i in (2, 3):
+            project(i, ["scalar_bank", "scalar_bank"])
+            store(i, [nc.scalar.copy, nc.scalar.copy])
+        transpose_ratio(6)
+        transpose_ratio(7)
+        gate(6, 0)
+        gate(6, 1)
+        for i in (4, 5):
+            project(i, ["scalar_bank", "scalar_bank"])
+            store(i, [nc.scalar.copy, nc.scalar.copy])
+        gate(7, 0)
+        quantise_g(6)
+        gate(7, 1)
+        quantise_g(7)
         for i in (6, 7):
             project(i, ["scalar_bank", "vector_bank"])
             store(i, [nc.scalar.copy, nc.vector.tensor_copy])

@@ -33,6 +33,8 @@ def tile_rwkv2timemix_pa_kernel(tc, x, time_mix, Wr, wkv, sum_k, Wo, out):
     ) as inputs, tc.tile_pool(name="keep", bufs=1) as keep, tc.tile_pool(
         name="work", bufs=4
     ) as work, tc.tile_pool(name="groups", bufs=6) as groups, tc.tile_pool(
+        name="early", bufs=1
+    ) as early, tc.tile_pool(
         name="gated", bufs=3
     ) as gated, tc.psum_pool(name="psum", bufs=4) as psum, tc.manual_schedule():
         ones = consts.tile([P, 1], F32, name="ones")
@@ -78,14 +80,23 @@ def tile_rwkv2timemix_pa_kernel(tc, x, time_mix, Wr, wkv, sum_k, Wo, out):
                     out=sk_sb[n][:, i : i + k, :], in_=sum_k_rows[rows, :].rearrange("(i p) c -> p i c", p=P)
                 )
 
+        def load_wo(n, c=None):
+            if n not in wo_sb:
+                wo_sb[n] = inputs.tile([P, 2, CH], BF16, name="wo" + str(n), tag="wo")
+            cols = slice(0, CH) if c is None else slice(HALF * c, HALF * (c + 1))
+            nc.sync.dma_start(
+                out=wo_sb[n][:, :, cols], in_=Wo[2 * P * n : 2 * P * (n + 1), cols].rearrange("(i p) c -> p i c", p=P)
+            )
+
         wr_sb, x_sb, sk_sb, wkv_sb, wo_sb = {}, {}, {}, {}, {}
         load_x(0, 0, 2)
+        load_wo(2, 0)
         load_sk(0, 2)
         load_x(0, 1)
         load_x(1, 0)
         load_sk(1)
         for n in range(2):
-            wo_sb[n] = load_pair(Wo, n, "wo")
+            load_wo(n)
         load_x(1, 1)
         for j in range(2):
             wr_sb[j] = load_wr(j)
@@ -93,8 +104,8 @@ def tile_rwkv2timemix_pa_kernel(tc, x, time_mix, Wr, wkv, sum_k, Wo, out):
         for j in range(2, 4):
             wr_sb[j] = load_wr(j)
         load_sk(3)
-        for n in range(2, 4):
-            wo_sb[n] = load_pair(Wo, n, "wo")
+        load_wo(2, 1)
+        load_wo(3)
         for n in range(4):
             wkv_sb[n] = load_pair(wkv_rows, n, "wkv")
 
@@ -181,30 +192,34 @@ def tile_rwkv2timemix_pa_kernel(tc, x, time_mix, Wr, wkv, sum_k, Wo, out):
         def quantise_x(half, c, grouped):
             quantise(grouped[:].rearrange("p k t -> p (k t)"), x_codes[:, half, c, :], x_scales[:, half, c, :])
 
-        def transpose_weight(pair, c, tag):
-            bank = psum.tile([P, 2, 2 * P], F32, name="w_bank", tag=tag)
+        def weight_tile(tag):
+            return (early if tag == "early" else groups).tile([P, 4 * HALF], BF16, name="w_grouped", tag=tag, align_bytes=64)
+
+        def weight_bank(grouped, b, pair, c, engine):
+            bank = psum.tile(
+                [P, 2, 2 * P], F32, name="w_bank", tag="scalar_bank" if engine is nc.scalar else "vector_bank"
+            )
             for u in range(2):
                 for m in range(2):
                     words = pair[:, m, :].bitcast(F32)
                     nc.tensor.transpose(
                         bank[:, u, P * m : P * (m + 1)], words[:, 2 * P * c + u : 2 * P * (c + 1) : 2], ident[:]
                     )
-            return bank
-
-        def group_weight(banks, copies):
-            grouped = groups.tile([P, 4 * HALF], BF16, name="w_grouped", tag="grouped", align_bytes=64)
+            copy = nc.scalar.copy if engine is nc.scalar else nc.vector.tensor_copy
             words = grouped[:].bitcast(F32).rearrange("p (b n u) -> p b n u", b=2, u=2)
-            for b in range(2):
-                copies[b](out=words[:, b, :, :], in_=banks[b][:].rearrange("p u n -> p n u"))
+            copy(out=words[:, b, :, :], in_=bank[:].rearrange("p u n -> p n u"))
+
+        def group_wr(j, engine):
+            grouped = weight_tile("grouped")
+            for c in range(PASSES):
+                weight_bank(grouped, c, wr_sb[j], c, engine)
             return grouped
 
-        def group_wr(j):
-            banks = [transpose_weight(wr_sb[j], c, "scalar_bank") for c in range(PASSES)]
-            return group_weight(banks, [nc.scalar.copy, nc.scalar.copy])
-
-        def group_wo(half, c, tag, copy):
-            banks = [transpose_weight(wo_sb[2 * half + m], c, tag) for m in range(2)]
-            return group_weight(banks, [copy, copy])
+        def group_wo(half, c, engine):
+            grouped = weight_tile("grouped")
+            for m in range(2):
+                weight_bank(grouped, m, wo_sb[2 * half + m], c, engine)
+            return grouped
 
         def quantise_wr(j, grouped):
             quantise(
@@ -323,9 +338,9 @@ def tile_rwkv2timemix_pa_kernel(tc, x, time_mix, Wr, wkv, sum_k, Wo, out):
                 copies[half](out=result[:, cols], in_=o_banks[i][half][:])
                 nc.sync.dma_start(out=out_rows[P * i : P * (i + 1), cols], in_=result[:, cols])
 
-        on_scalar = ("scalar_bank", nc.scalar.copy)
-        on_vector = ("vector_bank", nc.vector.tensor_copy)
         copy_x(0, 0, transpose_x(0, 0))
+        wo10 = weight_tile("early")
+        weight_bank(wo10, 0, wo_sb[2], 0, nc.vector)
         planes00 = mix(0, 0, scale_current(0, 0))
         reciprocal_root(0)
         reciprocal_root(1)
@@ -335,78 +350,78 @@ def tile_rwkv2timemix_pa_kernel(tc, x, time_mix, Wr, wkv, sum_k, Wo, out):
         copy_x(1, 0, transpose_x(1, 0))
         planes01 = mix(0, 1, scale_current(0, 1))
         reciprocal_root(2)
-        wo00 = group_wo(0, 0, *on_scalar)
+        wo00 = group_wo(0, 0, nc.scalar)
         planes10 = mix(1, 0, scale_current(1, 0))
         quantise_x(0, 0, x00)
         x01 = interleave(planes01)
         copy_x(1, 1, transpose_x(1, 1))
-        wo01 = group_wo(0, 1, *on_scalar)
+        wo01 = group_wo(0, 1, nc.scalar)
         planes11 = mix(1, 1, scale_current(1, 1))
         square(1)
         quantise_x(0, 1, x01)
         quantise_wo(0, 0, wo00)
-        wr0 = group_wr(0)
-        x10 = interleave(planes10)
         reciprocal_root(3)
-        wr1 = group_wr(1)
+        wr0 = group_wr(0, nc.scalar)
+        x10 = interleave(planes10)
+        wr1 = group_wr(1, nc.scalar)
         quantise_wo(0, 1, wo01)
         quantise_wr(0, wr0)
-        wr2 = group_wr(2)
+        wr2 = group_wr(2, nc.scalar)
         quantise_wr(1, wr1)
         quantise_x(1, 0, x10)
         reciprocal_root(4)
-        wr3 = group_wr(3)
+        wr3 = group_wr(3, nc.scalar)
         x11 = interleave(planes11)
         quantise_wr(2, wr2)
         divide(0)
         quantise_wr(3, wr3)
         quantise_x(1, 1, x11)
         divide(1)
-        wo10 = group_wo(1, 0, *on_vector)
+        weight_bank(wo10, 1, wo_sb[3], 0, nc.vector)
+        wo11 = group_wo(1, 1, nc.vector)
         receptance(0)
         for i in range(5, N_TILES):
             reciprocal_root(i)
+        quantise_wo(1, 0, wo10)
         transpose_ratio(0)
         transpose_ratio(1)
         sigmoid(0)
         gate(0, 0)
         gate(0, 1)
+        quantise_wo(1, 1, wo11)
         receptance(1)
-        quantise_wo(1, 0, wo10)
         square(2)
+        square(3)
         gate(1, 0)
         quantise_g(0)
         gate(1, 1)
         sigmoid(1)
-        wo11 = group_wo(1, 1, *on_vector)
         divide(2)
         quantise_g(1)
-        square(3)
         receptance(2)
-        quantise_wo(1, 1, wo11)
-        divide(3)
-        transpose_ratio(2)
         square(4)
         sigmoid(2)
+        divide(3)
+        transpose_ratio(2)
+        transpose_ratio(3)
         gate(2, 0)
         gate(2, 1)
-        transpose_ratio(3)
         square(5)
+        for i in (0, 1):
+            project(i, ["scalar_bank", "scalar_bank"])
+            store(i, [nc.scalar.copy, nc.scalar.copy])
         gate(3, 0)
         quantise_g(2)
         gate(3, 1)
-        receptance(3)
         square(6)
         divide(4)
         quantise_g(3)
         divide(5)
-        sigmoid(3)
         transpose_ratio(4)
-        transpose_ratio(5)
+        receptance(3)
         square(7)
-        for i in (0, 1):
-            project(i, ["scalar_bank", "scalar_bank"])
-            store(i, [nc.scalar.copy, nc.scalar.copy])
+        sigmoid(3)
+        transpose_ratio(5)
         gate(4, 0)
         gate(4, 1)
         divide(6)
@@ -419,12 +434,13 @@ def tile_rwkv2timemix_pa_kernel(tc, x, time_mix, Wr, wkv, sum_k, Wo, out):
             project(i, ["scalar_bank", "scalar_bank"])
             store(i, [nc.scalar.copy, nc.scalar.copy])
         transpose_ratio(6)
+        project(4, ["scalar_bank", "scalar_bank"])
+        store(4, [nc.scalar.copy, nc.scalar.copy])
         transpose_ratio(7)
         gate(6, 0)
         gate(6, 1)
-        for i in (4, 5):
-            project(i, ["scalar_bank", "scalar_bank"])
-            store(i, [nc.scalar.copy, nc.scalar.copy])
+        project(5, ["scalar_bank", "scalar_bank"])
+        store(5, [nc.scalar.copy, nc.scalar.copy])
         gate(7, 0)
         quantise_g(6)
         gate(7, 1)

@@ -80,12 +80,11 @@ def tile_rwkv2timemix_pa_kernel(tc, x, time_mix, Wr, wkv, sum_k, Wo, out):
                     out=sk_sb[n][:, i : i + k, :], in_=sum_k_rows[rows, :].rearrange("(i p) c -> p i c", p=P)
                 )
 
-        def load_wo(n, c=None):
-            if n not in wo_sb:
-                wo_sb[n] = inputs.tile([P, 2, CH], BF16, name="wo" + str(n), tag="wo")
-            cols = slice(0, CH) if c is None else slice(HALF * c, HALF * (c + 1))
+        def load_wo(n, c):
+            wo_sb[n, c] = inputs.tile([P, 2, HALF], BF16, name="wo" + str(n) + str(c), tag="wo")
             nc.sync.dma_start(
-                out=wo_sb[n][:, :, cols], in_=Wo[2 * P * n : 2 * P * (n + 1), cols].rearrange("(i p) c -> p i c", p=P)
+                out=wo_sb[n, c][:],
+                in_=Wo[2 * P * n : 2 * P * (n + 1), HALF * c : HALF * (c + 1)].rearrange("(i p) c -> p i c", p=P),
             )
 
         wr_sb, x_sb, sk_sb, wkv_sb, wo_sb = {}, {}, {}, {}, {}
@@ -96,7 +95,7 @@ def tile_rwkv2timemix_pa_kernel(tc, x, time_mix, Wr, wkv, sum_k, Wo, out):
         load_x(1, 0)
         load_sk(1)
         for n in range(2):
-            load_wo(n)
+            wo_sb[n] = load_pair(Wo, n, "wo")
         load_x(1, 1)
         for j in range(2):
             wr_sb[j] = load_wr(j)
@@ -104,10 +103,6 @@ def tile_rwkv2timemix_pa_kernel(tc, x, time_mix, Wr, wkv, sum_k, Wo, out):
         for j in range(2, 4):
             wr_sb[j] = load_wr(j)
         load_sk(3)
-        load_wo(2, 1)
-        load_wo(3)
-        for n in range(4):
-            wkv_sb[n] = load_pair(wkv_rows, n, "wkv")
 
         tm_col = consts.tile([P, 2 * 4], F32, name="tm_col")
         nc.vector.tensor_copy(out=tm_col[:], in_=tm_pairs[:].rearrange("p c t -> p (c t)"))
@@ -195,16 +190,14 @@ def tile_rwkv2timemix_pa_kernel(tc, x, time_mix, Wr, wkv, sum_k, Wo, out):
         def weight_tile(tag):
             return (early if tag == "early" else groups).tile([P, 4 * HALF], BF16, name="w_grouped", tag=tag, align_bytes=64)
 
-        def weight_bank(grouped, b, pair, c, engine):
+        def weight_bank(grouped, b, pair, engine):
             bank = psum.tile(
                 [P, 2, 2 * P], F32, name="w_bank", tag="scalar_bank" if engine is nc.scalar else "vector_bank"
             )
             for u in range(2):
                 for m in range(2):
                     words = pair[:, m, :].bitcast(F32)
-                    nc.tensor.transpose(
-                        bank[:, u, P * m : P * (m + 1)], words[:, 2 * P * c + u : 2 * P * (c + 1) : 2], ident[:]
-                    )
+                    nc.tensor.transpose(bank[:, u, P * m : P * (m + 1)], words[:, u : 2 * P : 2], ident[:])
             copy = nc.scalar.copy if engine is nc.scalar else nc.vector.tensor_copy
             words = grouped[:].bitcast(F32).rearrange("p (b n u) -> p b n u", b=2, u=2)
             copy(out=words[:, b, :, :], in_=bank[:].rearrange("p u n -> p n u"))
@@ -212,13 +205,16 @@ def tile_rwkv2timemix_pa_kernel(tc, x, time_mix, Wr, wkv, sum_k, Wo, out):
         def group_wr(j, engine):
             grouped = weight_tile("grouped")
             for c in range(PASSES):
-                weight_bank(grouped, c, wr_sb[j], c, engine)
+                weight_bank(grouped, c, wr_sb[j][:, :, HALF * c : HALF * (c + 1)], engine)
             return grouped
+
+        def wo_part(n, c):
+            return wo_sb[n, c][:] if (n, c) in wo_sb else wo_sb[n][:, :, HALF * c : HALF * (c + 1)]
 
         def group_wo(half, c, engine):
             grouped = weight_tile("grouped")
             for m in range(2):
-                weight_bank(grouped, m, wo_sb[2 * half + m], c, engine)
+                weight_bank(grouped, m, wo_part(2 * half + m, c), engine)
             return grouped
 
         def quantise_wr(j, grouped):
@@ -232,27 +228,30 @@ def tile_rwkv2timemix_pa_kernel(tc, x, time_mix, Wr, wkv, sum_k, Wo, out):
             cols = slice(HALF * half, HALF * (half + 1))
             quantise(grouped[:], wo_codes[:, c, cols], wo_scales[:, c, cols])
 
-        root = {}
         ratio = {}
 
-        def reciprocal_root(i):
-            root[i] = keep.tile([P, 4, PASSES, P], F32, name="root" + str(i))
+        def planes_of(i, tiles):
+            rows = slice(HALF // 8 * (i % 2), HALF // 8 * (i % 2 + tiles))
+            return ratio[i // 2][:].rearrange("p t i c (n k) -> p (i c n) t k", k=4)[:, rows, :, :]
+
+        def channels_of(pair, i, tiles):
+            rows = slice(HALF // 8 * (i % 2), HALF // 8 * (i % 2 + tiles))
+            return pair[:].rearrange("p i (n k t) -> p (i n) t k", k=4, t=4)[:, rows, :, :]
+
+        def reciprocal_root(i, tiles=1):
+            if i % 2 == 0:
+                ratio[i // 2] = keep.tile([P, 4, 2, PASSES, P], F32, name="ratio" + str(i // 2))
             nc.scalar.activation(
-                out=root[i][:].rearrange("p t c (n i) -> p (c n) t i", i=4),
-                in_=sk_sb[i // 2][:, i % 2, :].rearrange("p (n i t) -> p n t i", i=4, t=4),
-                func=ACT.Abs_reciprocal_sqrt,
+                out=planes_of(i, tiles), in_=channels_of(sk_sb[i // 2], i, tiles), func=ACT.Abs_reciprocal_sqrt
             )
 
-        def square(i):
-            nc.scalar.activation(out=root[i][:], in_=root[i][:], func=ACT.Square)
+        def square(i, tiles=1):
+            part = ratio[i // 2][:, :, i % 2 : i % 2 + tiles, :, :]
+            nc.scalar.activation(out=part, in_=part, func=ACT.Square)
 
         def divide(i):
-            ratio[i] = inputs.tile([P, 4, PASSES, P], F32, name="ratio" + str(i), tag=("x" if i % 4 < 2 else "sk"))
             nc.vector.tensor_tensor(
-                out=ratio[i][:].rearrange("p t c (n i) -> p (c n) t i", i=4),
-                in0=wkv_sb[i // 2][:, i % 2, :].rearrange("p (n i t) -> p n t i", i=4, t=4),
-                in1=root[i][:].rearrange("p t c (n i) -> p (c n) t i", i=4),
-                op=ALU.mult,
+                out=planes_of(i, 1), in0=channels_of(wkv_sb[i // 2], i, 1), in1=planes_of(i, 1), op=ALU.mult
             )
 
         gates = {}
@@ -288,7 +287,7 @@ def tile_rwkv2timemix_pa_kernel(tc, x, time_mix, Wr, wkv, sum_k, Wo, out):
             for c2 in range(PASSES):
                 bank = psum.tile([P, 4, P], F32, name="q_bank", tag="vector_bank")
                 for t in range(4):
-                    nc.tensor.transpose(bank[:, t, :], ratio[i][:, t, c2, :], ident[:])
+                    nc.tensor.transpose(bank[:, t, :], ratio[i // 2][:, t, i % 2, c2, :], ident[:])
                 banks.append(bank)
             ratio_banks[i] = banks
 
@@ -340,10 +339,13 @@ def tile_rwkv2timemix_pa_kernel(tc, x, time_mix, Wr, wkv, sum_k, Wo, out):
 
         copy_x(0, 0, transpose_x(0, 0))
         wo10 = weight_tile("early")
-        weight_bank(wo10, 0, wo_sb[2], 0, nc.vector)
+        weight_bank(wo10, 0, wo_part(2, 0), nc.vector)
+        load_wo(2, 1)
+        wo_sb[3] = load_pair(Wo, 3, "wo")
+        for n in range(4):
+            wkv_sb[n] = load_pair(wkv_rows, n, "wkv")
         planes00 = mix(0, 0, scale_current(0, 0))
-        reciprocal_root(0)
-        reciprocal_root(1)
+        reciprocal_root(0, 2)
         copy_x(0, 1, transpose_x(0, 1))
         x00 = interleave(planes00)
         square(0)
@@ -377,11 +379,11 @@ def tile_rwkv2timemix_pa_kernel(tc, x, time_mix, Wr, wkv, sum_k, Wo, out):
         quantise_wr(3, wr3)
         quantise_x(1, 1, x11)
         divide(1)
-        weight_bank(wo10, 1, wo_sb[3], 0, nc.vector)
+        weight_bank(wo10, 1, wo_part(3, 0), nc.vector)
         wo11 = group_wo(1, 1, nc.vector)
         receptance(0)
-        for i in range(5, N_TILES):
-            reciprocal_root(i)
+        reciprocal_root(5)
+        reciprocal_root(6, 2)
         quantise_wo(1, 0, wo10)
         transpose_ratio(0)
         transpose_ratio(1)
@@ -390,8 +392,7 @@ def tile_rwkv2timemix_pa_kernel(tc, x, time_mix, Wr, wkv, sum_k, Wo, out):
         gate(0, 1)
         quantise_wo(1, 1, wo11)
         receptance(1)
-        square(2)
-        square(3)
+        square(2, 2)
         gate(1, 0)
         quantise_g(0)
         gate(1, 1)
@@ -413,12 +414,12 @@ def tile_rwkv2timemix_pa_kernel(tc, x, time_mix, Wr, wkv, sum_k, Wo, out):
         gate(3, 0)
         quantise_g(2)
         gate(3, 1)
-        square(6)
         divide(4)
         quantise_g(3)
         divide(5)
         transpose_ratio(4)
         receptance(3)
+        square(6)
         square(7)
         sigmoid(3)
         transpose_ratio(5)

@@ -35,7 +35,7 @@ def tile_rwkv2timemix_pa_kernel(tc, x, time_mix, Wr, wkv, sum_k, Wo, out):
     ) as work, tc.tile_pool(name="groups", bufs=6) as groups, tc.tile_pool(
         name="early", bufs=1
     ) as early, tc.tile_pool(
-        name="gated", bufs=3
+        name="gated", bufs=2
     ) as gated, tc.psum_pool(name="psum", bufs=4) as psum, tc.manual_schedule():
         ones = consts.tile([P, 1], F32, name="ones")
         nc.vector.memset(ones[:], 1.0)
@@ -114,6 +114,9 @@ def tile_rwkv2timemix_pa_kernel(tc, x, time_mix, Wr, wkv, sum_k, Wo, out):
         for col in range(2 * 4):
             nc.vector.tensor_scalar_mul(out=tm_diag[:, col, :], in0=ident[:], scalar1=tm_col[:, col : col + 1])
 
+        less_diag = consts.tile([P, 2 * 4, P], BF16, name="less_diag")
+        nc.vector.tensor_scalar_mul(out=less_diag[:], in0=tm_diag[:], scalar1=-1.0)
+
         x_codes = keep.tile([P, 2, PASSES, HALF], U32, name="x_codes", align_bytes=64)
         x_scales = keep.tile([P, 2, PASSES, HALF], U8, name="x_scales", align_bytes=64)
         wr_codes = keep.tile([P, 4, PASSES, 2 * P], U32, name="wr_codes", align_bytes=64)
@@ -177,15 +180,47 @@ def tile_rwkv2timemix_pa_kernel(tc, x, time_mix, Wr, wkv, sum_k, Wo, out):
             return planes
 
         def interleave(planes):
-            grouped = groups.tile([P, HALF, 4], BF16, name="x_grouped", tag="grouped", align_bytes=64)
+            grouped = weight_tile("grouped")
             nc.vector.tensor_copy(
-                out=grouped[:].rearrange("p (n i) t -> p n t i", i=4),
+                out=grouped[:].rearrange("p (n i t) -> p n t i", i=4, t=4),
                 in_=planes[:].rearrange("p t (n i) -> p n t i", i=4),
             )
             return grouped
 
+        differences = {}
+
+        def scale_difference(half, c, tiles):
+            for k in tiles:
+                bank = psum.tile([P, 4, P], F32, name="x_difference", tag="vector_bank")
+                first = PAD + P * (k % 2)
+                for t in range(4):
+                    row = xt_pairs[half][:, c, t // 2, k // 2, :, t % 2]
+                    nc.tensor.matmul(
+                        out=bank[:, t, :], lhsT=tm_diag[:, 4 * c + t, :], rhs=row[:, first : first + P], start=True, stop=False
+                    )
+                    nc.tensor.matmul(
+                        out=bank[:, t, :],
+                        lhsT=less_diag[:, 4 * c + t, :],
+                        rhs=row[:, first - 1 : first - 1 + P],
+                        start=False,
+                        stop=True,
+                    )
+                differences[half, c, k] = bank
+
+        def add_previous(half, c):
+            grouped = weight_tile("grouped")
+            for k in range(4):
+                first = PAD - 1 + P * (k % 2)
+                nc.vector.tensor_tensor(
+                    out=grouped[:, 4 * P * k : 4 * P * (k + 1)].rearrange("p (n u e) -> p n u e", u=2, e=2),
+                    in0=xt_pairs[half][:, c, :, k // 2, first : first + P, :].rearrange("p u n e -> p n u e"),
+                    in1=differences[half, c, k][:].rearrange("p (u e) n -> p n u e", u=2),
+                    op=ALU.add,
+                )
+            return grouped
+
         def quantise_x(half, c, grouped):
-            quantise(grouped[:].rearrange("p k t -> p (k t)"), x_codes[:, half, c, :], x_scales[:, half, c, :])
+            quantise(grouped[:], x_codes[:, half, c, :], x_scales[:, half, c, :])
 
         def weight_tile(tag):
             return (early if tag == "early" else groups).tile([P, 4 * HALF], BF16, name="w_grouped", tag=tag, align_bytes=64)
@@ -202,10 +237,10 @@ def tile_rwkv2timemix_pa_kernel(tc, x, time_mix, Wr, wkv, sum_k, Wo, out):
             words = grouped[:].bitcast(F32).rearrange("p (b n u) -> p b n u", b=2, u=2)
             copy(out=words[:, b, :, :], in_=bank[:].rearrange("p u n -> p n u"))
 
-        def group_wr(j, engine):
+        def group_wr(j, engines):
             grouped = weight_tile("grouped")
             for c in range(PASSES):
-                weight_bank(grouped, c, wr_sb[j][:, :, HALF * c : HALF * (c + 1)], engine)
+                weight_bank(grouped, c, wr_sb[j][:, :, HALF * c : HALF * (c + 1)], engines[c])
             return grouped
 
         def wo_part(n, c):
@@ -342,8 +377,10 @@ def tile_rwkv2timemix_pa_kernel(tc, x, time_mix, Wr, wkv, sum_k, Wo, out):
         weight_bank(wo10, 0, wo_part(2, 0), nc.vector)
         load_wo(2, 1)
         wo_sb[3] = load_pair(Wo, 3, "wo")
-        for n in range(4):
-            wkv_sb[n] = load_pair(wkv_rows, n, "wkv")
+        wkv_sb[0] = load_pair(wkv_rows, 0, "wkv")
+        wkv_sb[1] = load_pair(wkv_rows, 1, "wkv")
+        wkv_sb[2] = load_pair(wkv_rows, 2, "wkv")
+        wkv_sb[3] = load_pair(wkv_rows, 3, "wkv")
         planes00 = mix(0, 0, scale_current(0, 0))
         reciprocal_root(0, 2)
         copy_x(0, 1, transpose_x(0, 1))
@@ -356,24 +393,25 @@ def tile_rwkv2timemix_pa_kernel(tc, x, time_mix, Wr, wkv, sum_k, Wo, out):
         planes10 = mix(1, 0, scale_current(1, 0))
         quantise_x(0, 0, x00)
         x01 = interleave(planes01)
+        square(1)
         copy_x(1, 1, transpose_x(1, 1))
         wo01 = group_wo(0, 1, nc.scalar)
-        planes11 = mix(1, 1, scale_current(1, 1))
-        square(1)
         quantise_x(0, 1, x01)
         quantise_wo(0, 0, wo00)
         reciprocal_root(3)
-        wr0 = group_wr(0, nc.scalar)
+        wr0 = group_wr(0, [nc.scalar, nc.scalar])
         x10 = interleave(planes10)
-        wr1 = group_wr(1, nc.scalar)
+        wr1 = group_wr(1, [nc.scalar, nc.scalar])
+        scale_difference(1, 1, (0, 1))
         quantise_wo(0, 1, wo01)
         quantise_wr(0, wr0)
-        wr2 = group_wr(2, nc.scalar)
+        wr2 = group_wr(2, [nc.scalar, nc.scalar])
+        scale_difference(1, 1, (2, 3))
         quantise_wr(1, wr1)
         quantise_x(1, 0, x10)
+        x11 = add_previous(1, 1)
         reciprocal_root(4)
-        wr3 = group_wr(3, nc.scalar)
-        x11 = interleave(planes11)
+        wr3 = group_wr(3, [nc.scalar, nc.scalar])
         quantise_wr(2, wr2)
         divide(0)
         quantise_wr(3, wr3)
@@ -408,9 +446,10 @@ def tile_rwkv2timemix_pa_kernel(tc, x, time_mix, Wr, wkv, sum_k, Wo, out):
         gate(2, 0)
         gate(2, 1)
         square(5)
-        for i in (0, 1):
-            project(i, ["scalar_bank", "scalar_bank"])
-            store(i, [nc.scalar.copy, nc.scalar.copy])
+        project(0, ["scalar_bank", "scalar_bank"])
+        store(0, [nc.scalar.copy, nc.scalar.copy])
+        project(1, ["scalar_bank", "scalar_bank"])
+        store(1, [nc.scalar.copy, nc.scalar.copy])
         gate(3, 0)
         quantise_g(2)
         gate(3, 1)
@@ -431,10 +470,11 @@ def tile_rwkv2timemix_pa_kernel(tc, x, time_mix, Wr, wkv, sum_k, Wo, out):
         gate(5, 1)
         divide(7)
         quantise_g(5)
-        for i in (2, 3):
-            project(i, ["scalar_bank", "scalar_bank"])
-            store(i, [nc.scalar.copy, nc.scalar.copy])
         transpose_ratio(6)
+        project(2, ["scalar_bank", "scalar_bank"])
+        store(2, [nc.scalar.copy, nc.scalar.copy])
+        project(3, ["scalar_bank", "scalar_bank"])
+        store(3, [nc.scalar.copy, nc.scalar.copy])
         project(4, ["scalar_bank", "scalar_bank"])
         store(4, [nc.scalar.copy, nc.scalar.copy])
         transpose_ratio(7)
@@ -446,6 +486,7 @@ def tile_rwkv2timemix_pa_kernel(tc, x, time_mix, Wr, wkv, sum_k, Wo, out):
         quantise_g(6)
         gate(7, 1)
         quantise_g(7)
-        for i in (6, 7):
-            project(i, ["scalar_bank", "vector_bank"])
-            store(i, [nc.scalar.copy, nc.vector.tensor_copy])
+        project(6, ["scalar_bank", "vector_bank"])
+        store(6, [nc.scalar.copy, nc.vector.tensor_copy])
+        project(7, ["scalar_bank", "vector_bank"])
+        store(7, [nc.scalar.copy, nc.vector.tensor_copy])

@@ -246,10 +246,10 @@ def tile_rwkv2timemix_pa_kernel(tc, x, time_mix, Wr, wkv, sum_k, Wo, out):
         def wo_part(n, c):
             return wo_sb[n, c][:] if (n, c) in wo_sb else wo_sb[n][:, :, HALF * c : HALF * (c + 1)]
 
-        def group_wo(half, c, engine):
+        def group_wo(half, c, engines):
             grouped = weight_tile("grouped")
             for m in range(2):
-                weight_bank(grouped, m, wo_part(2 * half + m, c), engine)
+                weight_bank(grouped, m, wo_part(2 * half + m, c), engines[m])
             return grouped
 
         def quantise_wr(j, grouped):
@@ -389,13 +389,13 @@ def tile_rwkv2timemix_pa_kernel(tc, x, time_mix, Wr, wkv, sum_k, Wo, out):
         copy_x(1, 0, transpose_x(1, 0))
         planes01 = mix(0, 1, scale_current(0, 1))
         reciprocal_root(2)
-        wo00 = group_wo(0, 0, nc.scalar)
+        wo00 = group_wo(0, 0, [nc.scalar, nc.vector])
         planes10 = mix(1, 0, scale_current(1, 0))
         quantise_x(0, 0, x00)
         x01 = interleave(planes01)
         square(1)
         copy_x(1, 1, transpose_x(1, 1))
-        wo01 = group_wo(0, 1, nc.scalar)
+        wo01 = group_wo(0, 1, [nc.scalar, nc.vector])
         quantise_x(0, 1, x01)
         quantise_wo(0, 0, wo00)
         reciprocal_root(3)
@@ -418,7 +418,7 @@ def tile_rwkv2timemix_pa_kernel(tc, x, time_mix, Wr, wkv, sum_k, Wo, out):
         quantise_x(1, 1, x11)
         divide(1)
         weight_bank(wo10, 1, wo_part(3, 0), nc.vector)
-        wo11 = group_wo(1, 1, nc.vector)
+        wo11 = group_wo(1, 1, [nc.vector, nc.vector])
         receptance(0)
         reciprocal_root(5)
         reciprocal_root(6, 2)

import concourse.mybir as mybir
from concourse.masks import make_identity

F32 = mybir.dt.float32
BF16 = mybir.dt.bfloat16
U32 = mybir.dt.uint32
U8 = mybir.dt.uint8
FP8X4 = mybir.dt.float8_e4m3fn_x4
ACT = mybir.ActivationFunctionType
ALU = mybir.AluOpType

P = 128
TOKENS = 1024
SEQ = 256
CH = 1024
PASSES = 2
HALF = 512
N_TILES = TOKENS // P
PAD = 8

FLOPS = 2 * 2 * TOKENS * CH * CH


def tile_rwkv2timemix_pa_kernel(tc, x, time_mix, Wr, wkv, sum_k, Wo, out):
    nc = tc.nc
    x_rows = x.flatten_outer_dims()
    wkv_rows = wkv.flatten_outer_dims()
    sum_k_rows = sum_k.flatten_outer_dims()
    out_rows = out.flatten_outer_dims()

    with tc.tile_pool(name="consts", bufs=1) as consts, tc.tile_pool(
        name="inputs", bufs=4
    ) as inputs, tc.tile_pool(name="keep", bufs=1) as keep, tc.tile_pool(
        name="work", bufs=4
    ) as work, tc.tile_pool(name="groups", bufs=6) as groups, tc.tile_pool(
        name="early", bufs=1
    ) as early, tc.tile_pool(
        name="gated", bufs=2
    ) as gated, tc.psum_pool(name="psum", bufs=4) as psum, tc.manual_schedule():
        ones = consts.tile([P, 1], F32, name="ones")
        nc.vector.memset(ones[:], 1.0)
        ident = consts.tile([P, P], F32, name="ident")
        make_identity(nc, ident[:])
        tm_pairs = consts.tile([P, PASSES, 4], BF16, name="tm_pairs")
        nc.scalar.dma_start(
            out=tm_pairs[:], in_=time_mix.squeeze().rearrange("(c p t) -> p c t", p=P, t=4)
        )
        warm = consts.tile([P, 1], F32, name="warm")
        nc.scalar.activation(out=warm[:], in_=ones[:], func=ACT.Abs_reciprocal_sqrt)

        def load_pair(rows, n, name):
            pair = inputs.tile([P, 2, CH], BF16, name=name + str(n), tag=name)
            nc.sync.dma_start(
                out=pair[:], in_=rows[2 * P * n : 2 * P * (n + 1), :].rearrange("(i p) c -> p i c", p=P)
            )
            return pair

        def load_wr(j):
            pair = inputs.tile([P, 2, CH], BF16, name="wr" + str(j), tag="wr")
            rows = Wr[HALF * (j // 2) : HALF * (j // 2 + 1), :].rearrange("(p t) c -> p t c", t=4)
            nc.sync.dma_start(out=pair[:], in_=rows[:, 2 * (j % 2) : 2 * (j % 2) + 2, :])
            return pair

        def load_x(half, c, pieces=1):
            x_sb[half, c] = inputs.tile([P, 4, HALF], BF16, name="x" + str(half) + str(c), tag="x")
            n = 4 // pieces
            for k in range(0, 4, n):
                rows = slice(HALF * half + P * k, HALF * half + P * (k + n))
                nc.sync.dma_start(
                    out=x_sb[half, c][:, k : k + n, :],
                    in_=x_rows[rows, HALF * c : HALF * (c + 1)].rearrange("(k p) c -> p k c", p=P),
                )

        def load_sk(n, pieces=1):
            sk_sb[n] = inputs.tile([P, 2, CH], BF16, name="sk" + str(n), tag="sk")
            k = 2 // pieces
            for i in range(0, 2, k):
                rows = slice(P * (2 * n + i), P * (2 * n + i + k))
                nc.sync.dma_start(
                    out=sk_sb[n][:, i : i + k, :], in_=sum_k_rows[rows, :].rearrange("(i p) c -> p i c", p=P)
                )

        def load_wo(n, c):
            wo_sb[n, c] = inputs.tile([P, 2, HALF], BF16, name="wo" + str(n) + str(c), tag="wo")
            nc.sync.dma_start(
                out=wo_sb[n, c][:],
                in_=Wo[2 * P * n : 2 * P * (n + 1), HALF * c : HALF * (c + 1)].rearrange("(i p) c -> p i c", p=P),
            )

        wr_sb, x_sb, sk_sb, wkv_sb, wo_sb = {}, {}, {}, {}, {}
        load_x(0, 0, 2)
        load_wo(2, 0)
        load_sk(0, 2)
        load_x(0, 1)
        load_x(1, 0)
        load_sk(1)
        for n in range(2):
            wo_sb[n] = load_pair(Wo, n, "wo")
        load_x(1, 1)
        for j in range(2):
            wr_sb[j] = load_wr(j)
        load_sk(2)
        for j in range(2, 4):
            wr_sb[j] = load_wr(j)
        load_sk(3)

        tm_col = consts.tile([P, 2 * 4], F32, name="tm_col")
        nc.vector.tensor_copy(out=tm_col[:], in_=tm_pairs[:].rearrange("p c t -> p (c t)"))
        rest_col = consts.tile([P, 2 * 4], F32, name="rest_col")
        nc.vector.tensor_scalar(
            out=rest_col[:], in0=tm_col[:], scalar1=-1.0, scalar2=1.0, op0=ALU.mult, op1=ALU.add
        )
        tm_diag = consts.tile([P, 2 * 4, P], BF16, name="tm_diag")
        for col in range(2 * 4):
            nc.vector.tensor_scalar_mul(out=tm_diag[:, col, :], in0=ident[:], scalar1=tm_col[:, col : col + 1])

        less_diag = consts.tile([P, 2 * 4, P], BF16, name="less_diag")
        nc.vector.tensor_scalar_mul(out=less_diag[:], in0=tm_diag[:], scalar1=-1.0)

        x_codes = keep.tile([P, 2, PASSES, HALF], U32, name="x_codes", align_bytes=64)
        x_scales = keep.tile([P, 2, PASSES, HALF], U8, name="x_scales", align_bytes=64)
        wr_codes = keep.tile([P, 4, PASSES, 2 * P], U32, name="wr_codes", align_bytes=64)
        wr_scales = keep.tile([P, 4, PASSES, 2 * P], U8, name="wr_scales", align_bytes=64)
        wo_codes = keep.tile([P, PASSES, CH], U32, name="wo_codes", align_bytes=64)
        wo_scales = keep.tile([P, PASSES, CH], U8, name="wo_scales", align_bytes=64)
        g_codes = keep.tile([P, N_TILES, PASSES, P], U32, name="g_codes", align_bytes=64)
        g_scales = keep.tile([P, N_TILES, PASSES, P], U8, name="g_scales", align_bytes=64)

        def quantise(grouped, codes, scales):
            nc.vector.quantize_mx(out=codes.bitcast(FP8X4), scales=scales, in_=grouped)

        xt_pairs = []
        xt_words = []
        for half in range(2):
            xt = keep.tile([P, PASSES, 2, 2, PAD + SEQ], F32, name="xt" + str(half))
            xt_words.append(xt)
            xt_pairs.append(xt[:].bitcast(BF16).rearrange("p c u s (k e) -> p c u s k e", e=2))
            nc.vector.memset(xt_pairs[half][:, :, :, :, 0:PAD, :], 0.0)

        def transpose_x(half, c):
            banks = []
            for s in range(2):
                bank = psum.tile([P, 2, SEQ], F32, name="x_bank", tag="scalar_bank")
                for k in range(2):
                    words = x_sb[half, c][:, 2 * s + k, :].bitcast(F32)
                    for u in range(2):
                        nc.tensor.transpose(bank[:, u, P * k : P * (k + 1)], words[:, u : 2 * P : 2], ident[:])
                banks.append(bank)
            return banks

        def copy_x(half, c, banks):
            for s in range(2):
                nc.scalar.copy(out=xt_words[half][:, c, :, s, PAD : PAD + SEQ], in_=banks[s][:])

        def scale_current(half, c):
            banks = []
            for t in range(4):
                scaled = psum.tile([P, 2, SEQ], F32, name="x_scaled", tag="vector_bank")
                nc.tensor.matmul(
                    out=scaled[:],
                    lhsT=tm_diag[:, 4 * c + t, :],
                    rhs=xt_pairs[half][:, c, t // 2, :, PAD : PAD + SEQ, t % 2],
                    start=True,
                    stop=True,
                )
                banks.append(scaled)
            return banks

        def mix(half, c, banks):
            planes = work.tile([P, 4, HALF], BF16, name="xm_planes", tag="planes")
            for t in range(4):
                nc.vector.scalar_tensor_tensor(
                    out=planes[:, t, :].rearrange("p (s k) -> p s k", s=2),
                    in0=xt_pairs[half][:, c, t // 2, :, PAD - 1 : PAD - 1 + SEQ, t % 2],
                    scalar=rest_col[:, 4 * c + t : 4 * c + t + 1],
                    in1=banks[t][:],
                    op0=ALU.mult,
                    op1=ALU.add,
                )
            return planes

        def interleave(planes):
            grouped = weight_tile("grouped")
            nc.vector.tensor_copy(
                out=grouped[:].rearrange("p (n i t) -> p n t i", i=4, t=4),
                in_=planes[:].rearrange("p t (n i) -> p n t i", i=4),
            )
            return grouped

        differences = {}

        def scale_difference(half, c, tiles):
            for k in tiles:
                bank = psum.tile([P, 4, P], F32, name="x_difference", tag="vector_bank")
                first = PAD + P * (k % 2)
                for t in range(4):
                    row = xt_pairs[half][:, c, t // 2, k // 2, :, t % 2]
                    nc.tensor.matmul(
                        out=bank[:, t, :], lhsT=tm_diag[:, 4 * c + t, :], rhs=row[:, first : first + P], start=True, stop=False
                    )
                    nc.tensor.matmul(
                        out=bank[:, t, :],
                        lhsT=less_diag[:, 4 * c + t, :],
                        rhs=row[:, first - 1 : first - 1 + P],
                        start=False,
                        stop=True,
                    )
                differences[half, c, k] = bank

        def add_previous(half, c):
            grouped = weight_tile("grouped")
            for k in range(4):
                first = PAD - 1 + P * (k % 2)
                nc.vector.tensor_tensor(
                    out=grouped[:, 4 * P * k : 4 * P * (k + 1)].rearrange("p (n u e) -> p n u e", u=2, e=2),
                    in0=xt_pairs[half][:, c, :, k // 2, first : first + P, :].rearrange("p u n e -> p n u e"),
                    in1=differences[half, c, k][:].rearrange("p (u e) n -> p n u e", u=2),
                    op=ALU.add,
                )
            return grouped

        def quantise_x(half, c, grouped):
            quantise(grouped[:], x_codes[:, half, c, :], x_scales[:, half, c, :])

        def weight_tile(tag):
            return (early if tag == "early" else groups).tile([P, 4 * HALF], BF16, name="w_grouped", tag=tag, align_bytes=64)

        def weight_bank(grouped, b, pair, engine):
            bank = psum.tile(
                [P, 2, 2 * P], F32, name="w_bank", tag="scalar_bank" if engine is nc.scalar else "vector_bank"
            )
            for u in range(2):
                for m in range(2):
                    words = pair[:, m, :].bitcast(F32)
                    nc.tensor.transpose(bank[:, u, P * m : P * (m + 1)], words[:, u : 2 * P : 2], ident[:])
            copy = nc.scalar.copy if engine is nc.scalar else nc.vector.tensor_copy
            words = grouped[:].bitcast(F32).rearrange("p (b n u) -> p b n u", b=2, u=2)
            copy(out=words[:, b, :, :], in_=bank[:].rearrange("p u n -> p n u"))

        def group_wr(j, engines):
            grouped = weight_tile("grouped")
            for c in range(PASSES):
                weight_bank(grouped, c, wr_sb[j][:, :, HALF * c : HALF * (c + 1)], engines[c])
            return grouped

        def wo_part(n, c):
            return wo_sb[n, c][:] if (n, c) in wo_sb else wo_sb[n][:, :, HALF * c : HALF * (c + 1)]

        def group_wo(half, c, engines):
            grouped = weight_tile("grouped")
            for m in range(2):
                weight_bank(grouped, m, wo_part(2 * half + m, c), engines[m])
            return grouped

        def quantise_wr(j, grouped):
            quantise(
                grouped[:],
                wr_codes[:, j, :, :].rearrange("p c n -> p (c n)"),
                wr_scales[:, j, :, :].rearrange("p c n -> p (c n)"),
            )

        def quantise_wo(half, c, grouped):
            cols = slice(HALF * half, HALF * (half + 1))
            quantise(grouped[:], wo_codes[:, c, cols], wo_scales[:, c, cols])

        ratio = {}

        def planes_of(i, tiles):
            rows = slice(HALF // 8 * (i % 2), HALF // 8 * (i % 2 + tiles))
            return ratio[i // 2][:].rearrange("p t i c (n k) -> p (i c n) t k", k=4)[:, rows, :, :]

        def channels_of(pair, i, tiles):
            rows = slice(HALF // 8 * (i % 2), HALF // 8 * (i % 2 + tiles))
            return pair[:].rearrange("p i (n k t) -> p (i n) t k", k=4, t=4)[:, rows, :, :]

        def reciprocal_root(i, tiles=1):
            if i % 2 == 0:
                ratio[i // 2] = keep.tile([P, 4, 2, PASSES, P], F32, name="ratio" + str(i // 2))
            nc.scalar.activation(
                out=planes_of(i, tiles), in_=channels_of(sk_sb[i // 2], i, tiles), func=ACT.Abs_reciprocal_sqrt
            )

        def square(i, tiles=1):
            part = ratio[i // 2][:, :, i % 2 : i % 2 + tiles, :, :]
            nc.scalar.activation(out=part, in_=part, func=ACT.Square)

        def divide(i):
            nc.vector.tensor_tensor(
                out=planes_of(i, 1), in0=channels_of(wkv_sb[i // 2], i, 1), in1=planes_of(i, 1), op=ALU.mult
            )

        gates = {}
        r_banks = {}

        def receptance(s):
            cols = slice(SEQ * (s % 2), SEQ * (s % 2 + 1))
            r_banks[s] = []
            for j in range(4):
                acc = psum.tile([P, 2, SEQ], F32, name="r_acc", tag="scalar_bank")
                for e in range(2):
                    for c in range(PASSES):
                        nc.tensor.matmul_mx(
                            out=acc[:, e, :],
                            lhsT=wr_codes[:, j, c, P * e : P * (e + 1)].bitcast(FP8X4),
                            lhsT_scale=wr_scales[:, j, c, P * e : P * (e + 1)],
                            rhs=x_codes[:, s // 2, c, cols].bitcast(FP8X4),
                            rhs_scale=x_scales[:, s // 2, c, cols],
                            start=(c == 0),
                            stop=(c == PASSES - 1),
                        )
                r_banks[s].append(acc)

        def sigmoid(s):
            gates[s] = work.tile([P, 2 * 4, SEQ], F32, name="sig", tag="planes")
            for j in range(4):
                nc.scalar.activation(out=gates[s][:, 2 * j : 2 * j + 2, :], in_=r_banks[s][j][:], func=ACT.Sigmoid)

        ratio_banks = {}

        def transpose_ratio(i):
            banks = []
            for c2 in range(PASSES):
                bank = psum.tile([P, 4, P], F32, name="q_bank", tag="vector_bank")
                for t in range(4):
                    nc.tensor.transpose(bank[:, t, :], ratio[i // 2][:, t, i % 2, c2, :], ident[:])
                banks.append(bank)
            ratio_banks[i] = banks

        g_grouped = {}

        def gate(i, c2):
            if c2 == 0:
                g_grouped[i] = gated.tile([P, PASSES, P, 4], BF16, name="g_grouped", tag="g_grouped", align_bytes=64)
            cols = slice(P * (i % 2), P * (i % 2 + 1))
            nc.vector.tensor_tensor(
                out=g_grouped[i][:, c2, :, :].rearrange("p (n i) t -> p n t i", i=4),
                in0=gates[i // 2][:, 4 * c2 : 4 * (c2 + 1), cols].rearrange("p t (n i) -> p n t i", i=4),
                in1=ratio_banks[i][c2][:].rearrange("p t (n i) -> p n t i", i=4),
                op=ALU.mult,
            )

        def quantise_g(i):
            quantise(
                g_grouped[i][:].rearrange("p c k t -> p (c k t)"),
                g_codes[:, i, :, :].rearrange("p c k -> p (c k)"),
                g_scales[:, i, :, :].rearrange("p c k -> p (c k)"),
            )

        o_banks = {}

        def project(i, tags):
            o_banks[i] = []
            for half in range(2):
                cols = slice(HALF * half, HALF * (half + 1))
                acc = psum.tile([P, HALF], F32, name="o_acc", tag=tags[half])
                for c2 in range(PASSES):
                    nc.tensor.matmul_mx(
                        out=acc[:],
                        lhsT=g_codes[:, i, c2, :].bitcast(FP8X4),
                        lhsT_scale=g_scales[:, i, c2, :],
                        rhs=wo_codes[:, c2, cols].bitcast(FP8X4),
                        rhs_scale=wo_scales[:, c2, cols],
                        start=(c2 == 0),
                        stop=(c2 == PASSES - 1),
                    )
                o_banks[i].append(acc)

        def store(i, copies):
            result = inputs.tile([P, CH], F32, name="result", tag="wr")
            for half in range(2):
                cols = slice(HALF * half, HALF * (half + 1))
                copies[half](out=result[:, cols], in_=o_banks[i][half][:])
                nc.sync.dma_start(out=out_rows[P * i : P * (i + 1), cols], in_=result[:, cols])

        copy_x(0, 0, transpose_x(0, 0))
        wo10 = weight_tile("early")
        weight_bank(wo10, 0, wo_part(2, 0), nc.vector)
        load_wo(2, 1)
        wo_sb[3] = load_pair(Wo, 3, "wo")
        wkv_sb[0] = load_pair(wkv_rows, 0, "wkv")
        wkv_sb[1] = load_pair(wkv_rows, 1, "wkv")
        wkv_sb[2] = load_pair(wkv_rows, 2, "wkv")
        wkv_sb[3] = load_pair(wkv_rows, 3, "wkv")
        planes00 = mix(0, 0, scale_current(0, 0))
        reciprocal_root(0, 2)
        copy_x(0, 1, transpose_x(0, 1))
        x00 = interleave(planes00)
        square(0)
        copy_x(1, 0, transpose_x(1, 0))
        planes01 = mix(0, 1, scale_current(0, 1))
        reciprocal_root(2)
        wo00 = group_wo(0, 0, [nc.scalar, nc.vector])
        planes10 = mix(1, 0, scale_current(1, 0))
        quantise_x(0, 0, x00)
        x01 = interleave(planes01)
        square(1)
        copy_x(1, 1, transpose_x(1, 1))
        wo01 = group_wo(0, 1, [nc.scalar, nc.vector])
        quantise_x(0, 1, x01)
        quantise_wo(0, 0, wo00)
        reciprocal_root(3)
        wr0 = group_wr(0, [nc.scalar, nc.scalar])
        x10 = interleave(planes10)
        wr1 = group_wr(1, [nc.scalar, nc.scalar])
        scale_difference(1, 1, (0, 1))
        quantise_wo(0, 1, wo01)
        quantise_wr(0, wr0)
        wr2 = group_wr(2, [nc.scalar, nc.scalar])
        scale_difference(1, 1, (2, 3))
        quantise_wr(1, wr1)
        quantise_x(1, 0, x10)
        x11 = add_previous(1, 1)
        reciprocal_root(4)
        wr3 = group_wr(3, [nc.scalar, nc.scalar])
        quantise_wr(2, wr2)
        divide(0)
        quantise_wr(3, wr3)
        quantise_x(1, 1, x11)
        divide(1)
        weight_bank(wo10, 1, wo_part(3, 0), nc.vector)
        wo11 = group_wo(1, 1, [nc.vector, nc.vector])
        receptance(0)
        reciprocal_root(5)
        reciprocal_root(6, 2)
        quantise_wo(1, 0, wo10)
        transpose_ratio(0)
        transpose_ratio(1)
        sigmoid(0)
        gate(0, 0)
        gate(0, 1)
        quantise_wo(1, 1, wo11)
        receptance(1)
        square(2, 2)
        gate(1, 0)
        quantise_g(0)
        gate(1, 1)
        sigmoid(1)
        divide(2)
        quantise_g(1)
        receptance(2)
        square(4)
        sigmoid(2)
        divide(3)
        transpose_ratio(2)
        transpose_ratio(3)
        gate(2, 0)
        gate(2, 1)
        square(5)
        project(0, ["scalar_bank", "scalar_bank"])
        store(0, [nc.scalar.copy, nc.scalar.copy])
        project(1, ["scalar_bank", "scalar_bank"])
        store(1, [nc.scalar.copy, nc.scalar.copy])
        gate(3, 0)
        quantise_g(2)
        gate(3, 1)
        divide(4)
        quantise_g(3)
        divide(5)
        transpose_ratio(4)
        receptance(3)
        square(6)
        square(7)
        sigmoid(3)
        transpose_ratio(5)
        gate(4, 0)
        gate(4, 1)
        divide(6)
        gate(5, 0)
        quantise_g(4)
        gate(5, 1)
        divide(7)
        quantise_g(5)
        transpose_ratio(6)
        project(2, ["scalar_bank", "scalar_bank"])
        store(2, [nc.scalar.copy, nc.scalar.copy])
        project(3, ["scalar_bank", "scalar_bank"])
        store(3, [nc.scalar.copy, nc.scalar.copy])
        project(4, ["scalar_bank", "scalar_bank"])
        store(4, [nc.scalar.copy, nc.scalar.copy])
        transpose_ratio(7)
        gate(6, 0)
        gate(6, 1)
        project(5, ["scalar_bank", "scalar_bank"])
        store(5, [nc.scalar.copy, nc.scalar.copy])
        gate(7, 0)
        quantise_g(6)
        gate(7, 1)
        quantise_g(7)
        project(6, ["scalar_bank", "vector_bank"])
        store(6, [nc.scalar.copy, nc.vector.tensor_copy])
        project(7, ["scalar_bank", "vector_bank"])
        store(7, [nc.scalar.copy, nc.vector.tensor_copy])
